import numpy as np
import ml_dtypes


def mxq(x, axis, fmt="e4m3"):
    dtype, down = {"e4m3": (ml_dtypes.float8_e4m3fn, 7), "e5m2": (ml_dtypes.float8_e5m2, 14)}[fmt]
    v = np.moveaxis(np.asarray(x, np.float32).astype(ml_dtypes.bfloat16).astype(np.float64), axis, -1)
    blocks = v.reshape(v.shape[:-1] + (-1, 32))
    amax = np.abs(blocks).max(-1, keepdims=True)
    byte = np.maximum(np.where(amax > 0, np.frexp(amax)[1] - 1 + 127, 0) - down, 1)
    scale = np.exp2(byte - 127.0)
    codes = (blocks / scale).astype(np.float32).astype(dtype).astype(np.float64)
    return np.moveaxis((codes * scale).reshape(v.shape), -1, axis)


WIDE = False


def mx_kscale(k):
    if not WIDE:
        return np.ones(k)
    levels = np.array([10, -10, 5, -5, 0])
    a = np.random.permutation(np.resize(levels, k // 512 * 4)).reshape(k // 512, 4)
    idx = np.arange(k)
    return np.exp2(a[idx // 512, idx % 128 // 32])


BF16 = ml_dtypes.bfloat16


def bf(x):
    return np.asarray(x, np.float32).astype(BF16)


def f64(x):
    return np.asarray(x).astype(np.float64)


E2M1 = np.array([0.0, 0.5, 1.0, 1.5, 2.0, 3.0, 4.0, 6.0, -0.0, -0.5, -1.0, -1.5, -2.0, -3.0, -4.0, -6.0])


def pack_weight(w, fmt):
    k, n = w.shape
    w = f64(bf(w)).reshape(k // 32, 32, n)
    amax = np.abs(w).max(1)
    if fmt == "e4m3":
        byte = np.frexp(amax)[1] - 1 + 127 - 7
    else:
        mant, ex = np.frexp(amax / 6.0)
        byte = np.where(mant > 0.5, ex, ex - 1) + 127
    byte = np.clip(np.where(amax > 0, byte, 1), 1, 254)
    scaled = (w * np.exp2(127.0 - byte)[:, None, :]).reshape(k, n).astype(np.float32)
    by_word = np.ascontiguousarray(scaled.reshape(k // 512, 128, 4, n).transpose(0, 1, 3, 2))
    if fmt == "e4m3":
        words = by_word.astype(ml_dtypes.float8_e4m3fn).view(np.uint8)
    else:
        c = by_word.astype(ml_dtypes.float4_e2m1fn).view(np.uint8) & 0xF
        words = c[..., 0::2] | (c[..., 1::2] << 4)
    return np.ascontiguousarray(words), np.ascontiguousarray(byte.astype(np.uint8).reshape(k // 512, 16, n))


def unpack_weight(words, scales, fmt):
    g, p, n, _ = words.shape
    if fmt == "e4m3":
        vals = np.ascontiguousarray(words).view(ml_dtypes.float8_e4m3fn).astype(np.float64)
    else:
        nib = np.empty((g, p, n, 4), np.uint8)
        nib[..., 0::2] = words & 0xF
        nib[..., 1::2] = words >> 4
        vals = E2M1[nib]
    vals = vals * np.repeat(np.exp2(scales.astype(np.float64) - 127.0), 8, axis=1)[..., None]
    return vals.transpose(0, 1, 3, 2).reshape(g * 512, n)

def pack4(w):
    words, scales = pack_weight(w, "e2m1")
    return words.reshape(words.shape[0], 128, -1), scales


def unpack4(words, scales):
    return unpack_weight(words.reshape(words.shape[0], 128, -1, 2), scales, "e2m1")


B, S, I, Hd = 3, 512, 128, 512


def sigmoid(v):
    return 1.0 / (1.0 + np.exp(-v))


def setup_inputs():
    t = mx_kscale(Hd)
    x = bf(np.random.standard_normal((B, S, I)))
    w_emb = bf(np.random.standard_normal((Hd, I)) / np.sqrt(I) * t[:, None])
    b_emb = bf(np.random.standard_normal(Hd) * 0.5 * t)
    w_ih = np.random.standard_normal((3 * Hd, Hd)) / np.sqrt(Hd) / t[None, :]
    w_ih_words, w_ih_scales = pack4(np.ascontiguousarray(w_ih.T))
    b_ih = bf(np.random.standard_normal(3 * Hd) * 0.5)
    b_hh = bf(np.random.standard_normal(3 * Hd))
    return {"x": x,
            "w_emb": w_emb,
            "b_emb": b_emb,
            "w_ih_words": w_ih_words,
            "w_ih_scales": w_ih_scales,
            "b_ih": b_ih,
            "b_hh": b_hh}


def reference(x, w_emb, b_emb, w_ih_words, w_ih_scales, b_ih, b_hh):
    emb = f64(x) @ f64(w_emb).T + f64(b_emb)
    gi = (mxq(emb, 2, "e4m3") @ unpack4(w_ih_words, w_ih_scales)) + f64(b_ih)
    ir, iz, inn = np.split(gi, 3, axis=-1)
    b_hr, b_hz, b_hn = np.split(f64(b_hh), 3)
    r = sigmoid(ir + b_hr)
    z = sigmoid(iz + b_hz)
    n = np.tanh(inn + r * b_hn)
    h = (1.0 - z) * n
    H = h[:, :-1, :]
    h_last = h[:, -1, :][None]
    return (H, h_last)

@@ -1,0 +1,217 @@
+from contextlib import ExitStack
+
+import concourse.mybir as mybir
+from concourse.masks import make_identity
+
+BF16 = mybir.dt.bfloat16
+F32 = mybir.dt.float32
+I32 = mybir.dt.int32
+U32 = mybir.dt.uint32
+U8 = mybir.dt.uint8
+FP8X4 = mybir.dt.float8_e4m3fn_x4
+FP4X4 = mybir.dt.float4_e2m1fn_x4
+ACT = mybir.ActivationFunctionType
+ALU = mybir.AluOpType
+
+P = 128
+PACK = 4
+BATCH = 3
+STEPS = 512
+IN = 128
+HID = 512
+GROUPS = STEPS // P
+HID_TILES = HID // P
+GATE_TILES = 3 * HID_TILES
+R = 0
+Z = 1
+N = 2
+
+FLOPS = 2 * BATCH * STEPS * IN * HID + 2 * BATCH * STEPS * HID * 3 * HID
+
+RAGGED_PIECES = ((0, 64), (64, 32), (96, 16), (112, 15))
+
+
+def tile_encoderrnn_kernel(tc, x, w_emb, b_emb, w_ih_words, w_ih_scales, b_ih, b_hh, out_0, out_1):
+    nc = tc.nc
+    with ExitStack() as stack:
+        keep = stack.enter_context(tc.tile_pool(name="keep", bufs=1))
+        work = stack.enter_context(tc.tile_pool(name="work", bufs=3))
+        pair = stack.enter_context(tc.tile_pool(name="pair", bufs=2))
+        psum = stack.enter_context(tc.psum_pool(name="psum", bufs=8))
+
+        x_sb = keep.tile([P, BATCH, GROUPS, IN], BF16)
+        w_sb = keep.tile([P, PACK, IN], BF16)
+        b_emb_sb = keep.tile([P, PACK], BF16)
+        w_words = keep.tile([P, 2 * 3 * HID], U8, align_bytes=64)
+        w_plane = keep.tile([P, 3 * HID], U8, align_bytes=64)
+        bias_rows = keep.tile([P, P], BF16)
+
+        nc.vector.memset(w_plane[:].bitcast(I32), 0)
+        nc.vector.memset(bias_rows[:], 0.0)
+
+        nc.sync.dma_start(out=w_sb[:], in_=w_emb.rearrange("(p t) i -> p t i", t=PACK))
+        nc.sync.dma_start(out=x_sb[:, 0], in_=x[0].rearrange("(p n) i -> p n i", n=GROUPS))
+        nc.sync.dma_start(out=b_emb_sb[:], in_=b_emb.rearrange("(p t) -> p t", t=PACK))
+        nc.sync.dma_start(out=w_words[:].bitcast(I32), in_=w_ih_words[0].bitcast(I32))
+        for quadrant in range(4):
+            nc.sync.dma_start(
+                out=w_plane[32 * quadrant : 32 * quadrant + 4, :].bitcast(I32),
+                in_=w_ih_scales[0, 4 * quadrant : 4 * quadrant + 4, :].bitcast(I32),
+            )
+        nc.sync.dma_start(out=bias_rows[0:GATE_TILES, :], in_=b_ih.rearrange("(m q) -> m q", q=P))
+        nc.sync.dma_start(out=bias_rows[GATE_TILES : 2 * GATE_TILES, :], in_=b_hh.rearrange("(m q) -> m q", q=P))
+        for b in range(1, BATCH):
+            nc.sync.dma_start(out=x_sb[:, b], in_=x[b].rearrange("(p n) i -> p n i", n=GROUPS))
+
+        ident_bf = keep.tile([P, P], BF16)
+        make_identity(nc, ident_bf[:])
+        ident_f32 = keep.tile([P, P], F32)
+        make_identity(nc, ident_f32[:])
+
+        warm = keep.tile([P, 1], F32)
+        nc.vector.memset(warm[:], 0.0)
+        nc.scalar.activation(out=warm[:], in_=warm[:], func=ACT.Sigmoid)
+
+        w_t_ps = psum.tile([P, PACK, P], BF16, tag="bank")
+        for t in range(PACK):
+            nc.tensor.transpose(w_t_ps[:, t, :], w_sb[:, t, :], ident_bf[:])
+        w_t = keep.tile([P, PACK, P], BF16)
+        nc.scalar.copy(out=w_t[:], in_=w_t_ps[:])
+
+        x_t = keep.tile([P, BATCH, STEPS], BF16)
+
+        def transpose_x(b):
+            x_t_ps = psum.tile([P, GROUPS, P], BF16, tag="bank")
+            for n in range(GROUPS):
+                nc.tensor.transpose(x_t_ps[:, n, :], x_sb[:, b, n, :], ident_bf[:])
+            nc.scalar.copy(out=x_t[:, b, :], in_=x_t_ps[:].rearrange("i n p -> i (n p)"))
+
+        emb_codes = keep.tile([P, BATCH, STEPS], U32, align_bytes=64)
+        emb_plane = keep.tile([P, BATCH, STEPS], U8, align_bytes=64)
+        grouped_of = {}
+
+        def embed_group(b, n):
+            if n == 0:
+                grouped = pair.tile([P, GROUPS, P, PACK], BF16, align_bytes=64)
+                grouped_of[b] = grouped
+            emb_ps = psum.tile([P, PACK, P], F32, tag="bank")
+            for t in range(PACK):
+                nc.tensor.matmul(
+                    emb_ps[:, t, :],
+                    lhsT=w_t[:, t, :],
+                    rhs=x_t[:, b, n * P : (n + 1) * P],
+                    start=True,
+                    stop=True,
+                )
+            nc.vector.tensor_tensor(
+                out=grouped_of[b][:, n],
+                in0=emb_ps[:].rearrange("p t s -> p s t"),
+                in1=b_emb_sb[:].unsqueeze(1).to_broadcast([P, P, PACK]),
+                op=ALU.add,
+            )
+
+        def quantise(b):
+            nc.vector.quantize_mx(
+                out=emb_codes[:, b, :].bitcast(FP8X4),
+                scales=emb_plane[:, b, :],
+                in_=grouped_of[b][:].rearrange("p n s t -> p (n s t)"),
+            )
+
+        transpose_x(0)
+        for n in range(GROUPS):
+            embed_group(0, n)
+        quantise(0)
+        for b in range(1, BATCH):
+            transpose_x(b)
+
+        bias_ps = psum.tile([P, P], BF16, tag="bank")
+        nc.tensor.transpose(bias_ps[:], bias_rows[:], ident_bf[:])
+        bias_cols = keep.tile([P, 2 * GATE_TILES], F32)
+        nc.vector.tensor_copy(out=bias_cols[:], in_=bias_ps[:, 0 : 2 * GATE_TILES])
+        b_in = bias_cols[:, N * HID_TILES : (N + 1) * HID_TILES]
+        b_hn = bias_cols[:, GATE_TILES + N * HID_TILES : GATE_TILES + (N + 1) * HID_TILES]
+        b_r = keep.tile([P, HID_TILES], F32)
+        nc.vector.tensor_add(
+            out=b_r[:], in0=bias_cols[:, 0:HID_TILES], in1=bias_cols[:, GATE_TILES : GATE_TILES + HID_TILES]
+        )
+        b_z = keep.tile([P, HID_TILES], F32)
+        nc.vector.tensor_add(
+            out=b_z[:],
+            in0=bias_cols[:, HID_TILES : 2 * HID_TILES],
+            in1=bias_cols[:, GATE_TILES + HID_TILES : GATE_TILES + 2 * HID_TILES],
+        )
+        minus_b_z = keep.tile([P, HID_TILES], F32)
+        nc.vector.tensor_scalar_mul(out=minus_b_z[:], in0=b_z[:], scalar1=-1.0)
+
+        def gate_pass(b, gate, j):
+            m = gate * HID_TILES + j
+            gate_ps = psum.tile([P, STEPS], F32, tag="bank")
+            nc.tensor.matmul_mx(
+                out=gate_ps[:],
+                lhsT=w_words[:, 2 * P * m : 2 * P * (m + 1)].bitcast(FP4X4),
+                lhsT_scale=w_plane[:, P * m : P * (m + 1)],
+                rhs=emb_codes[:, b, :].bitcast(FP8X4),
+                rhs_scale=emb_plane[:, b, :],
+                start=True,
+                stop=True,
+            )
+            return gate_ps
+
+        keep_of = {}
+        h_t_of = {}
+
+        def gates(b, j):
+            r_ps = gate_pass(b, R, j)
+            z_ps = gate_pass(b, Z, j)
+            n_ps = gate_pass(b, N, j)
+            r_sb = work.tile([P, STEPS], F32)
+            nc.scalar.activation(out=r_sb[:], in_=r_ps[:], func=ACT.Sigmoid, bias=b_r[:, j : j + 1], scale=1.0)
+            one_minus_z = work.tile([P, STEPS], F32)
+            nc.scalar.activation(
+                out=one_minus_z[:], in_=z_ps[:], func=ACT.Sigmoid, bias=minus_b_z[:, j : j + 1], scale=-1.0
+            )
+            pre_n = work.tile([P, STEPS], F32)
+            nc.vector.scalar_tensor_tensor(
+                out=pre_n[:], in0=r_sb[:], scalar=b_hn[:, j : j + 1], in1=n_ps[:], op0=ALU.mult, op1=ALU.add
+            )
+            keep_of[(b, j)] = (one_minus_z, pre_n)
+
+        def finish(b, j):
+            one_minus_z, pre_n = keep_of[(b, j)]
+            if j == 0:
+                h_t = pair.tile([P, HID_TILES, STEPS], F32)
+                h_t_of[b] = h_t
+            n_sb = work.tile([P, STEPS], F32)
+            nc.scalar.activation(out=n_sb[:], in_=pre_n[:], func=ACT.Tanh, bias=b_in[:, j : j + 1], scale=1.0)
+            nc.gpsimd.tensor_mul(out=h_t_of[b][:, j, :], in0=one_minus_z[:], in1=n_sb[:])
+
+        def emit(b, n):
+            h_ps = psum.tile([P, HID], F32, tag="bank")
+            for j in range(HID_TILES):
+                nc.tensor.transpose(h_ps[:, j * P : (j + 1) * P], h_t_of[b][:, j, n * P : (n + 1) * P], ident_f32[:])
+            h_sb = work.tile([P, HID], F32)
+            nc.vector.tensor_copy(out=h_sb[:], in_=h_ps[:])
+            if n < GROUPS - 1:
+                nc.sync.dma_start(out=out_0[b, n : STEPS - 1 : GROUPS, :], in_=h_sb[:])
+            else:
+                for first, count in RAGGED_PIECES:
+                    nc.sync.dma_start(
+                        out=out_0[b, GROUPS * first + n : GROUPS * (first + count) : GROUPS, :],
+                        in_=h_sb[first : first + count, :],
+                    )
+                nc.sync.dma_start(out=out_1[0, b : b + 1, :], in_=h_sb[P - 1 : P, :])
+
+        for step in range(BATCH * HID_TILES):
+            b, j = divmod(step, HID_TILES)
+            gates(b, j)
+            if b + 1 < BATCH:
+                embed_group(b + 1, j)
+                if j == GROUPS - 1:
+                    quantise(b + 1)
+            if step > 0:
+                finish(*divmod(step - 1, HID_TILES))
+            if b > 0:
+                emit(b - 1, (j + GROUPS - 1) % GROUPS)
+        finish(BATCH - 1, HID_TILES - 1)
+        for j in range(GROUPS):
+            emit(BATCH - 1, (j + GROUPS - 1) % GROUPS)

@@ -30,6 +30,8 @@ FLOPS = 2 * BATCH * STEPS * IN * HID + 2 * BATCH * STEPS * HID * 3 * HID
 
 RAGGED_PIECES = ((0, 64), (64, 32), (96, 16), (112, 15))
 
+EMIT_LAG = 5
+
 
 def tile_encoderrnn_kernel(tc, x, w_emb, b_emb, w_ih_words, w_ih_scales, b_ih, b_hh, out_0, out_1):
     nc = tc.nc
@@ -45,13 +47,17 @@ def tile_encoderrnn_kernel(tc, x, w_emb, b_emb, w_ih_words, w_ih_scales, b_ih, b
         w_words = keep.tile([P, 2 * 3 * HID], U8, align_bytes=64)
         w_plane = keep.tile([P, 3 * HID], U8, align_bytes=64)
         bias_rows = keep.tile([P, P], BF16)
+        warm = keep.tile([P, 1], F32)
 
         nc.vector.memset(w_plane[:].bitcast(I32), 0)
         nc.vector.memset(bias_rows[:], 0.0)
+        nc.vector.memset(warm[:], 0.0)
 
-        nc.sync.dma_start(out=w_sb[:], in_=w_emb.rearrange("(p t) i -> p t i", t=PACK))
         nc.sync.dma_start(out=x_sb[:, 0], in_=x[0].rearrange("(p n) i -> p n i", n=GROUPS))
+        nc.scalar.dma_start(out=w_sb[:], in_=w_emb.rearrange("(p t) i -> p t i", t=PACK))
         nc.sync.dma_start(out=b_emb_sb[:], in_=b_emb.rearrange("(p t) -> p t", t=PACK))
+        for b in range(1, BATCH):
+            nc.scalar.dma_start(out=x_sb[:, b], in_=x[b].rearrange("(p n) i -> p n i", n=GROUPS))
         nc.sync.dma_start(out=w_words[:].bitcast(I32), in_=w_ih_words[0].bitcast(I32))
         for quadrant in range(4):
             nc.sync.dma_start(
@@ -60,23 +66,19 @@ def tile_encoderrnn_kernel(tc, x, w_emb, b_emb, w_ih_words, w_ih_scales, b_ih, b
             )
         nc.sync.dma_start(out=bias_rows[0:GATE_TILES, :], in_=b_ih.rearrange("(m q) -> m q", q=P))
         nc.sync.dma_start(out=bias_rows[GATE_TILES : 2 * GATE_TILES, :], in_=b_hh.rearrange("(m q) -> m q", q=P))
-        for b in range(1, BATCH):
-            nc.sync.dma_start(out=x_sb[:, b], in_=x[b].rearrange("(p n) i -> p n i", n=GROUPS))
 
         ident_bf = keep.tile([P, P], BF16)
         make_identity(nc, ident_bf[:])
         ident_f32 = keep.tile([P, P], F32)
         make_identity(nc, ident_f32[:])
 
-        warm = keep.tile([P, 1], F32)
-        nc.vector.memset(warm[:], 0.0)
         nc.scalar.activation(out=warm[:], in_=warm[:], func=ACT.Sigmoid)
 
         w_t_ps = psum.tile([P, PACK, P], BF16, tag="bank")
         for t in range(PACK):
             nc.tensor.transpose(w_t_ps[:, t, :], w_sb[:, t, :], ident_bf[:])
         w_t = keep.tile([P, PACK, P], BF16)
-        nc.scalar.copy(out=w_t[:], in_=w_t_ps[:])
+        nc.vector.tensor_copy(out=w_t[:], in_=w_t_ps[:])
 
         x_t = keep.tile([P, BATCH, STEPS], BF16)
 
@@ -109,39 +111,39 @@ def tile_encoderrnn_kernel(tc, x, w_emb, b_emb, w_ih_words, w_ih_scales, b_ih, b
                 in1=b_emb_sb[:].unsqueeze(1).to_broadcast([P, P, PACK]),
                 op=ALU.add,
             )
-
-        def quantise(b):
-            nc.vector.quantize_mx(
-                out=emb_codes[:, b, :].bitcast(FP8X4),
-                scales=emb_plane[:, b, :],
-                in_=grouped_of[b][:].rearrange("p n s t -> p (n s t)"),
-            )
+            if n == GROUPS - 1:
+                nc.vector.quantize_mx(
+                    out=emb_codes[:, b, :].bitcast(FP8X4),
+                    scales=emb_plane[:, b, :],
+                    in_=grouped_of[b][:].rearrange("p n s t -> p (n s t)"),
+                )
 
         transpose_x(0)
         for n in range(GROUPS):
             embed_group(0, n)
-        quantise(0)
         for b in range(1, BATCH):
             transpose_x(b)
 
         bias_ps = psum.tile([P, P], BF16, tag="bank")
         nc.tensor.transpose(bias_ps[:], bias_rows[:], ident_bf[:])
         bias_cols = keep.tile([P, 2 * GATE_TILES], F32)
-        nc.vector.tensor_copy(out=bias_cols[:], in_=bias_ps[:, 0 : 2 * GATE_TILES])
+        nc.scalar.copy(out=bias_cols[:], in_=bias_ps[:, 0 : 2 * GATE_TILES])
+        minus_cols = keep.tile([P, 2 * GATE_TILES], F32)
+        nc.scalar.mul(out=minus_cols[:], in_=bias_ps[:, 0 : 2 * GATE_TILES], mul=-1.0)
         b_in = bias_cols[:, N * HID_TILES : (N + 1) * HID_TILES]
         b_hn = bias_cols[:, GATE_TILES + N * HID_TILES : GATE_TILES + (N + 1) * HID_TILES]
         b_r = keep.tile([P, HID_TILES], F32)
-        nc.vector.tensor_add(
-            out=b_r[:], in0=bias_cols[:, 0:HID_TILES], in1=bias_cols[:, GATE_TILES : GATE_TILES + HID_TILES]
-        )
-        b_z = keep.tile([P, HID_TILES], F32)
-        nc.vector.tensor_add(
-            out=b_z[:],
-            in0=bias_cols[:, HID_TILES : 2 * HID_TILES],
-            in1=bias_cols[:, GATE_TILES + HID_TILES : GATE_TILES + 2 * HID_TILES],
+        nc.gpsimd.tensor_add(
+            out=b_r[:],
+            in0=bias_cols[:, R * HID_TILES : (R + 1) * HID_TILES],
+            in1=bias_cols[:, GATE_TILES + R * HID_TILES : GATE_TILES + (R + 1) * HID_TILES],
         )
         minus_b_z = keep.tile([P, HID_TILES], F32)
-        nc.vector.tensor_scalar_mul(out=minus_b_z[:], in0=b_z[:], scalar1=-1.0)
+        nc.gpsimd.tensor_add(
+            out=minus_b_z[:],
+            in0=minus_cols[:, Z * HID_TILES : (Z + 1) * HID_TILES],
+            in1=minus_cols[:, GATE_TILES + Z * HID_TILES : GATE_TILES + (Z + 1) * HID_TILES],
+        )
 
         def gate_pass(b, gate, j):
             m = gate * HID_TILES + j
@@ -157,7 +159,7 @@ def tile_encoderrnn_kernel(tc, x, w_emb, b_emb, w_ih_words, w_ih_scales, b_ih, b
             )
             return gate_ps
 
-        keep_of = {}
+        halves_of = {}
         h_t_of = {}
 
         def gates(b, j):
@@ -174,23 +176,26 @@ def tile_encoderrnn_kernel(tc, x, w_emb, b_emb, w_ih_words, w_ih_scales, b_ih, b
             nc.vector.scalar_tensor_tensor(
                 out=pre_n[:], in0=r_sb[:], scalar=b_hn[:, j : j + 1], in1=n_ps[:], op0=ALU.mult, op1=ALU.add
             )
-            keep_of[(b, j)] = (one_minus_z, pre_n)
+            halves_of[(b, j)] = (one_minus_z, pre_n)
 
-        def finish(b, j):
-            one_minus_z, pre_n = keep_of[(b, j)]
+        def finish(b, j, product_engine):
+            one_minus_z, pre_n = halves_of[(b, j)]
             if j == 0:
                 h_t = pair.tile([P, HID_TILES, STEPS], F32)
                 h_t_of[b] = h_t
             n_sb = work.tile([P, STEPS], F32)
             nc.scalar.activation(out=n_sb[:], in_=pre_n[:], func=ACT.Tanh, bias=b_in[:, j : j + 1], scale=1.0)
-            nc.gpsimd.tensor_mul(out=h_t_of[b][:, j, :], in0=one_minus_z[:], in1=n_sb[:])
+            product_engine.tensor_mul(out=h_t_of[b][:, j, :], in0=one_minus_z[:], in1=n_sb[:])
 
-        def emit(b, n):
-            h_ps = psum.tile([P, HID], F32, tag="bank")
-            for j in range(HID_TILES):
-                nc.tensor.transpose(h_ps[:, j * P : (j + 1) * P], h_t_of[b][:, j, n * P : (n + 1) * P], ident_f32[:])
+        def transpose_back(h_ps, b, n, j):
+            nc.tensor.transpose(h_ps[:, j * P : (j + 1) * P], h_t_of[b][:, j, n * P : (n + 1) * P], ident_f32[:])
+
+        def store_group(h_ps, b, n, on_scalar):
             h_sb = work.tile([P, HID], F32)
-            nc.vector.tensor_copy(out=h_sb[:], in_=h_ps[:])
+            if on_scalar:
+                nc.scalar.copy(out=h_sb[:], in_=h_ps[:])
+            else:
+                nc.vector.tensor_copy(out=h_sb[:], in_=h_ps[:])
             if n < GROUPS - 1:
                 nc.sync.dma_start(out=out_0[b, n : STEPS - 1 : GROUPS, :], in_=h_sb[:])
             else:
@@ -201,17 +206,37 @@ def tile_encoderrnn_kernel(tc, x, w_emb, b_emb, w_ih_words, w_ih_scales, b_ih, b
                     )
                 nc.sync.dma_start(out=out_1[0, b : b + 1, :], in_=h_sb[P - 1 : P, :])
 
+        def group_in_turn(turn):
+            return (turn + GROUPS - 1) % GROUPS
+
+        def emit(turn):
+            b = turn // GROUPS
+            n = group_in_turn(turn)
+            h_ps = psum.tile([P, HID], F32, tag="bank")
+            for j in range(HID_TILES):
+                transpose_back(h_ps, b, n, j)
+            store_group(h_ps, b, n, on_scalar=False)
+
         for step in range(BATCH * HID_TILES):
-            b, j = divmod(step, HID_TILES)
-            gates(b, j)
-            if b + 1 < BATCH:
-                embed_group(b + 1, j)
-                if j == GROUPS - 1:
-                    quantise(b + 1)
-            if step > 0:
-                finish(*divmod(step - 1, HID_TILES))
-            if b > 0:
-                emit(b - 1, (j + GROUPS - 1) % GROUPS)
-        finish(BATCH - 1, HID_TILES - 1)
-        for j in range(GROUPS):
-            emit(BATCH - 1, (j + GROUPS - 1) % GROUPS)
+            if step < HID_TILES:
+                for later in (2 * step, 2 * step + 1):
+                    embed_group(1 + later // GROUPS, later % GROUPS)
+            gates(step // HID_TILES, step % HID_TILES)
+            if step >= 1:
+                finish((step - 1) // HID_TILES, (step - 1) % HID_TILES, nc.gpsimd)
+            if step >= EMIT_LAG:
+                emit(step - EMIT_LAG)
+        for turn in range(BATCH * HID_TILES - EMIT_LAG, (BATCH - 1) * GROUPS):
+            emit(turn)
+
+        last = BATCH - 1
+        last_ps = []
+        for turn in range(GROUPS):
+            h_ps = psum.tile([P, HID], F32, tag="bank")
+            last_ps.append(h_ps)
+            for j in range(HID_TILES - 1):
+                transpose_back(h_ps, last, group_in_turn(turn), j)
+        finish(last, HID_TILES - 1, nc.vector)
+        for turn in range(GROUPS):
+            transpose_back(last_ps[turn], last, group_in_turn(turn), HID_TILES - 1)
+            store_group(last_ps[turn], last, group_in_turn(turn), on_scalar=(turn % 2 == 1))

@@ -40,6 +40,7 @@ def tile_encoderrnn_kernel(tc, x, w_emb, b_emb, w_ih_words, w_ih_scales, b_ih, b
         work = stack.enter_context(tc.tile_pool(name="work", bufs=3))
         pair = stack.enter_context(tc.tile_pool(name="pair", bufs=2))
         psum = stack.enter_context(tc.psum_pool(name="psum", bufs=8))
+        stack.enter_context(tc.manual_schedule())
 
         x_sb = keep.tile([P, BATCH, GROUPS, IN], BF16)
         w_sb = keep.tile([P, PACK, IN], BF16)

@@ -19,30 +19,42 @@ BATCH = 3
 STEPS = 512
 IN = 128
 HID = 512
-GROUPS = STEPS // P
-HID_TILES = HID // P
-GATE_TILES = 3 * HID_TILES
+PER_BATCH = STEPS // P
+GROUPS = BATCH * PER_BATCH
+TILES = HID // P
+GATE_TILES = 3 * TILES
 R = 0
 Z = 1
 N = 2
+
+CHUNK_GROUPS = (2, 4, 4, 2)
+CHUNK_FIRST = (0, 2, 6, 10)
+assert sum(CHUNK_GROUPS) == GROUPS
+
+EMIT_LAG = 7
 
 FLOPS = 2 * BATCH * STEPS * IN * HID + 2 * BATCH * STEPS * HID * 3 * HID
 
 RAGGED_PIECES = ((0, 64), (64, 32), (96, 16), (112, 15))
 
-EMIT_LAG = 5
+
+def batch_of(g):
+    return g // PER_BATCH
+
+
+def n_of(g):
+    return (g + PER_BATCH - 1) % PER_BATCH
 
 
 def tile_encoderrnn_kernel(tc, x, w_emb, b_emb, w_ih_words, w_ih_scales, b_ih, b_hh, out_0, out_1):
     nc = tc.nc
     with ExitStack() as stack:
         keep = stack.enter_context(tc.tile_pool(name="keep", bufs=1))
-        work = stack.enter_context(tc.tile_pool(name="work", bufs=3))
-        pair = stack.enter_context(tc.tile_pool(name="pair", bufs=2))
+        work = stack.enter_context(tc.tile_pool(name="work", bufs=4))
+        leave = stack.enter_context(tc.tile_pool(name="leave", bufs=6))
         psum = stack.enter_context(tc.psum_pool(name="psum", bufs=8))
-        stack.enter_context(tc.manual_schedule())
 
-        x_sb = keep.tile([P, BATCH, GROUPS, IN], BF16)
+        x_sb = keep.tile([P, BATCH, PER_BATCH, IN], BF16)
         w_sb = keep.tile([P, PACK, IN], BF16)
         b_emb_sb = keep.tile([P, PACK], BF16)
         w_words = keep.tile([P, 2 * 3 * HID], U8, align_bytes=64)
@@ -54,11 +66,11 @@ def tile_encoderrnn_kernel(tc, x, w_emb, b_emb, w_ih_words, w_ih_scales, b_ih, b
         nc.vector.memset(bias_rows[:], 0.0)
         nc.vector.memset(warm[:], 0.0)
 
-        nc.sync.dma_start(out=x_sb[:, 0], in_=x[0].rearrange("(p n) i -> p n i", n=GROUPS))
+        nc.sync.dma_start(out=x_sb[:, 0], in_=x[0].rearrange("(p n) i -> p n i", n=PER_BATCH))
         nc.scalar.dma_start(out=w_sb[:], in_=w_emb.rearrange("(p t) i -> p t i", t=PACK))
         nc.sync.dma_start(out=b_emb_sb[:], in_=b_emb.rearrange("(p t) -> p t", t=PACK))
         for b in range(1, BATCH):
-            nc.scalar.dma_start(out=x_sb[:, b], in_=x[b].rearrange("(p n) i -> p n i", n=GROUPS))
+            nc.scalar.dma_start(out=x_sb[:, b], in_=x[b].rearrange("(p n) i -> p n i", n=PER_BATCH))
         nc.sync.dma_start(out=w_words[:].bitcast(I32), in_=w_ih_words[0].bitcast(I32))
         for quadrant in range(4):
             nc.sync.dma_start(
@@ -81,47 +93,46 @@ def tile_encoderrnn_kernel(tc, x, w_emb, b_emb, w_ih_words, w_ih_scales, b_ih, b
         w_t = keep.tile([P, PACK, P], BF16)
         nc.vector.tensor_copy(out=w_t[:], in_=w_t_ps[:])
 
-        x_t = keep.tile([P, BATCH, STEPS], BF16)
+        x_t = keep.tile([P, GROUPS, P], BF16)
 
         def transpose_x(b):
-            x_t_ps = psum.tile([P, GROUPS, P], BF16, tag="bank")
-            for n in range(GROUPS):
-                nc.tensor.transpose(x_t_ps[:, n, :], x_sb[:, b, n, :], ident_bf[:])
-            nc.scalar.copy(out=x_t[:, b, :], in_=x_t_ps[:].rearrange("i n p -> i (n p)"))
+            x_t_ps = psum.tile([P, PER_BATCH, P], BF16, tag="bank")
+            for turn in range(PER_BATCH):
+                nc.tensor.transpose(x_t_ps[:, turn, :], x_sb[:, b, n_of(turn), :], ident_bf[:])
+            nc.scalar.copy(out=x_t[:, b * PER_BATCH : (b + 1) * PER_BATCH, :], in_=x_t_ps[:])
 
-        emb_codes = keep.tile([P, BATCH, STEPS], U32, align_bytes=64)
-        emb_plane = keep.tile([P, BATCH, STEPS], U8, align_bytes=64)
-        grouped_of = {}
+        grouped = keep.tile([P, GROUPS, P, PACK], BF16, align_bytes=64)
+        emb_codes = keep.tile([P, GROUPS * P], U32, align_bytes=64)
+        emb_plane = keep.tile([P, GROUPS * P], U8, align_bytes=64)
 
-        def embed_group(b, n):
-            if n == 0:
-                grouped = pair.tile([P, GROUPS, P, PACK], BF16, align_bytes=64)
-                grouped_of[b] = grouped
+        def embed_group(g):
             emb_ps = psum.tile([P, PACK, P], F32, tag="bank")
             for t in range(PACK):
-                nc.tensor.matmul(
-                    emb_ps[:, t, :],
-                    lhsT=w_t[:, t, :],
-                    rhs=x_t[:, b, n * P : (n + 1) * P],
-                    start=True,
-                    stop=True,
-                )
+                nc.tensor.matmul(emb_ps[:, t, :], lhsT=w_t[:, t, :], rhs=x_t[:, g, :], start=True, stop=True)
             nc.vector.tensor_tensor(
-                out=grouped_of[b][:, n],
+                out=grouped[:, g],
                 in0=emb_ps[:].rearrange("p t s -> p s t"),
                 in1=b_emb_sb[:].unsqueeze(1).to_broadcast([P, P, PACK]),
                 op=ALU.add,
             )
-            if n == GROUPS - 1:
-                nc.vector.quantize_mx(
-                    out=emb_codes[:, b, :].bitcast(FP8X4),
-                    scales=emb_plane[:, b, :],
-                    in_=grouped_of[b][:].rearrange("p n s t -> p (n s t)"),
-                )
+
+        def quantise_chunk(c):
+            first, count = CHUNK_FIRST[c], CHUNK_GROUPS[c]
+            nc.vector.quantize_mx(
+                out=emb_codes[:, first * P : (first + count) * P].bitcast(FP8X4),
+                scales=emb_plane[:, first * P : (first + count) * P],
+                in_=grouped[:, first : first + count].rearrange("p g s t -> p (g s t)"),
+            )
+
+        def embed_and_quantise(g):
+            embed_group(g)
+            for c in range(len(CHUNK_GROUPS)):
+                if g == CHUNK_FIRST[c] + CHUNK_GROUPS[c] - 1:
+                    quantise_chunk(c)
 
         transpose_x(0)
-        for n in range(GROUPS):
-            embed_group(0, n)
+        for g in range(CHUNK_GROUPS[0]):
+            embed_and_quantise(g)
         for b in range(1, BATCH):
             transpose_x(b)
 
@@ -131,113 +142,113 @@ def tile_encoderrnn_kernel(tc, x, w_emb, b_emb, w_ih_words, w_ih_scales, b_ih, b
         nc.scalar.copy(out=bias_cols[:], in_=bias_ps[:, 0 : 2 * GATE_TILES])
         minus_cols = keep.tile([P, 2 * GATE_TILES], F32)
         nc.scalar.mul(out=minus_cols[:], in_=bias_ps[:, 0 : 2 * GATE_TILES], mul=-1.0)
-        b_in = bias_cols[:, N * HID_TILES : (N + 1) * HID_TILES]
-        b_hn = bias_cols[:, GATE_TILES + N * HID_TILES : GATE_TILES + (N + 1) * HID_TILES]
-        b_r = keep.tile([P, HID_TILES], F32)
+        b_in = bias_cols[:, N * TILES : (N + 1) * TILES]
+        b_hn = bias_cols[:, GATE_TILES + N * TILES : GATE_TILES + (N + 1) * TILES]
+        b_r = keep.tile([P, TILES], F32)
         nc.gpsimd.tensor_add(
             out=b_r[:],
-            in0=bias_cols[:, R * HID_TILES : (R + 1) * HID_TILES],
-            in1=bias_cols[:, GATE_TILES + R * HID_TILES : GATE_TILES + (R + 1) * HID_TILES],
+            in0=bias_cols[:, R * TILES : (R + 1) * TILES],
+            in1=bias_cols[:, GATE_TILES + R * TILES : GATE_TILES + (R + 1) * TILES],
         )
-        minus_b_z = keep.tile([P, HID_TILES], F32)
+        minus_b_z = keep.tile([P, TILES], F32)
         nc.gpsimd.tensor_add(
             out=minus_b_z[:],
-            in0=minus_cols[:, Z * HID_TILES : (Z + 1) * HID_TILES],
-            in1=minus_cols[:, GATE_TILES + Z * HID_TILES : GATE_TILES + (Z + 1) * HID_TILES],
+            in0=minus_cols[:, Z * TILES : (Z + 1) * TILES],
+            in1=minus_cols[:, GATE_TILES + Z * TILES : GATE_TILES + (Z + 1) * TILES],
         )
 
-        def gate_pass(b, gate, j):
-            m = gate * HID_TILES + j
-            gate_ps = psum.tile([P, STEPS], F32, tag="bank")
+        def columns_of(c):
+            return slice(CHUNK_FIRST[c] * P, (CHUNK_FIRST[c] + CHUNK_GROUPS[c]) * P)
+
+        def gate_pass(c, gate, j):
+            m = gate * TILES + j
+            gate_ps = psum.tile([P, CHUNK_GROUPS[c] * P], F32, tag="bank")
             nc.tensor.matmul_mx(
                 out=gate_ps[:],
                 lhsT=w_words[:, 2 * P * m : 2 * P * (m + 1)].bitcast(FP4X4),
                 lhsT_scale=w_plane[:, P * m : P * (m + 1)],
-                rhs=emb_codes[:, b, :].bitcast(FP8X4),
-                rhs_scale=emb_plane[:, b, :],
+                rhs=emb_codes[:, columns_of(c)].bitcast(FP8X4),
+                rhs_scale=emb_plane[:, columns_of(c)],
                 start=True,
                 stop=True,
             )
             return gate_ps
 
         halves_of = {}
-        h_t_of = {}
+        h_t = keep.tile([P, TILES, GROUPS * P], F32)
 
-        def gates(b, j):
-            r_ps = gate_pass(b, R, j)
-            z_ps = gate_pass(b, Z, j)
-            n_ps = gate_pass(b, N, j)
-            r_sb = work.tile([P, STEPS], F32)
+        def gates(c, j):
+            width = CHUNK_GROUPS[c] * P
+            r_ps = gate_pass(c, R, j)
+            z_ps = gate_pass(c, Z, j)
+            n_ps = gate_pass(c, N, j)
+            r_sb = work.tile([P, width], F32)
             nc.scalar.activation(out=r_sb[:], in_=r_ps[:], func=ACT.Sigmoid, bias=b_r[:, j : j + 1], scale=1.0)
-            one_minus_z = work.tile([P, STEPS], F32)
+            one_minus_z = work.tile([P, width], F32)
             nc.scalar.activation(
                 out=one_minus_z[:], in_=z_ps[:], func=ACT.Sigmoid, bias=minus_b_z[:, j : j + 1], scale=-1.0
             )
-            pre_n = work.tile([P, STEPS], F32)
+            pre_n = work.tile([P, width], F32)
             nc.vector.scalar_tensor_tensor(
                 out=pre_n[:], in0=r_sb[:], scalar=b_hn[:, j : j + 1], in1=n_ps[:], op0=ALU.mult, op1=ALU.add
             )
-            halves_of[(b, j)] = (one_minus_z, pre_n)
+            halves_of[(c, j)] = (one_minus_z, pre_n)
 
-        def finish(b, j, product_engine):
-            one_minus_z, pre_n = halves_of[(b, j)]
-            if j == 0:
-                h_t = pair.tile([P, HID_TILES, STEPS], F32)
-                h_t_of[b] = h_t
-            n_sb = work.tile([P, STEPS], F32)
+        def finish(c, j, product_engine):
+            one_minus_z, pre_n = halves_of[(c, j)]
+            n_sb = work.tile([P, CHUNK_GROUPS[c] * P], F32)
             nc.scalar.activation(out=n_sb[:], in_=pre_n[:], func=ACT.Tanh, bias=b_in[:, j : j + 1], scale=1.0)
-            product_engine.tensor_mul(out=h_t_of[b][:, j, :], in0=one_minus_z[:], in1=n_sb[:])
+            product_engine.tensor_mul(out=h_t[:, j, columns_of(c)], in0=one_minus_z[:], in1=n_sb[:])
 
-        def transpose_back(h_ps, b, n, j):
-            nc.tensor.transpose(h_ps[:, j * P : (j + 1) * P], h_t_of[b][:, j, n * P : (n + 1) * P], ident_f32[:])
+        def transpose_back(h_ps, g, j):
+            nc.tensor.transpose(h_ps[:, j * P : (j + 1) * P], h_t[:, j, g * P : (g + 1) * P], ident_f32[:])
 
-        def store_group(h_ps, b, n, on_scalar):
-            h_sb = work.tile([P, HID], F32)
+        def store_group(h_ps, g, first_tile, n_tiles, on_scalar):
+            b, n = batch_of(g), n_of(g)
+            cols = slice(first_tile * P, (first_tile + n_tiles) * P)
+            h_sb = leave.tile([P, n_tiles * P], F32)
             if on_scalar:
-                nc.scalar.copy(out=h_sb[:], in_=h_ps[:])
+                nc.scalar.copy(out=h_sb[:], in_=h_ps[:, cols])
             else:
-                nc.vector.tensor_copy(out=h_sb[:], in_=h_ps[:])
-            if n < GROUPS - 1:
-                nc.sync.dma_start(out=out_0[b, n : STEPS - 1 : GROUPS, :], in_=h_sb[:])
+                nc.vector.tensor_copy(out=h_sb[:], in_=h_ps[:, cols])
+            if n < PER_BATCH - 1:
+                nc.sync.dma_start(out=out_0[b, n : STEPS - 1 : PER_BATCH, cols], in_=h_sb[:])
             else:
                 for first, count in RAGGED_PIECES:
                     nc.sync.dma_start(
-                        out=out_0[b, GROUPS * first + n : GROUPS * (first + count) : GROUPS, :],
+                        out=out_0[b, PER_BATCH * first + n : PER_BATCH * (first + count) : PER_BATCH, cols],
                         in_=h_sb[first : first + count, :],
                     )
-                nc.sync.dma_start(out=out_1[0, b : b + 1, :], in_=h_sb[P - 1 : P, :])
+                nc.sync.dma_start(out=out_1[0, b : b + 1, cols], in_=h_sb[P - 1 : P, :])
 
-        def group_in_turn(turn):
-            return (turn + GROUPS - 1) % GROUPS
-
-        def emit(turn):
-            b = turn // GROUPS
-            n = group_in_turn(turn)
+        def emit(g, on_scalar):
             h_ps = psum.tile([P, HID], F32, tag="bank")
-            for j in range(HID_TILES):
-                transpose_back(h_ps, b, n, j)
-            store_group(h_ps, b, n, on_scalar=False)
+            for j in range(TILES):
+                transpose_back(h_ps, g, j)
+            store_group(h_ps, g, 0, TILES, on_scalar)
 
-        for step in range(BATCH * HID_TILES):
-            if step < HID_TILES:
-                for later in (2 * step, 2 * step + 1):
-                    embed_group(1 + later // GROUPS, later % GROUPS)
-            gates(step // HID_TILES, step % HID_TILES)
+        n_steps = len(CHUNK_GROUPS) * TILES
+        last = len(CHUNK_GROUPS) - 1
+        for step in range(n_steps):
+            if CHUNK_GROUPS[0] + step < GROUPS:
+                embed_and_quantise(CHUNK_GROUPS[0] + step)
+            gates(step // TILES, step % TILES)
             if step >= 1:
-                finish((step - 1) // HID_TILES, (step - 1) % HID_TILES, nc.gpsimd)
+                finish((step - 1) // TILES, (step - 1) % TILES, nc.gpsimd)
             if step >= EMIT_LAG:
-                emit(step - EMIT_LAG)
-        for turn in range(BATCH * HID_TILES - EMIT_LAG, (BATCH - 1) * GROUPS):
-            emit(turn)
+                emit(step - EMIT_LAG, on_scalar=False)
 
-        last = BATCH - 1
-        last_ps = []
-        for turn in range(GROUPS):
+        finish(last, TILES - 1, nc.vector)
+        for g in range(n_steps - EMIT_LAG, CHUNK_FIRST[last]):
+            emit(g, on_scalar=(g % 2 == 1))
+        last_groups = range(CHUNK_FIRST[last], GROUPS)
+        last_ps = {}
+        for g in last_groups:
             h_ps = psum.tile([P, HID], F32, tag="bank")
-            last_ps.append(h_ps)
-            for j in range(HID_TILES - 1):
-                transpose_back(h_ps, last, group_in_turn(turn), j)
-        finish(last, HID_TILES - 1, nc.vector)
-        for turn in range(GROUPS):
-            transpose_back(last_ps[turn], last, group_in_turn(turn), HID_TILES - 1)
-            store_group(last_ps[turn], last, group_in_turn(turn), on_scalar=(turn % 2 == 1))
+            last_ps[g] = h_ps
+            for j in range(TILES - 1):
+                transpose_back(h_ps, g, j)
+            store_group(h_ps, g, 0, TILES - 1, on_scalar=(g % 2 == 1))
+        for g in last_groups:
+            transpose_back(last_ps[g], g, TILES - 1)
+            store_group(last_ps[g], g, TILES - 1, 1, on_scalar=(g % 2 == 1))

@@ -33,6 +33,9 @@ assert sum(CHUNK_GROUPS) == GROUPS
 
 EMIT_LAG = 7
 
+SCALAR_EMBEDS = (1, 3)
+EMBEDS_AHEAD = 4
+
 FLOPS = 2 * BATCH * STEPS * IN * HID + 2 * BATCH * STEPS * HID * 3 * HID
 
 RAGGED_PIECES = ((0, 64), (64, 32), (96, 16), (112, 15))
@@ -85,6 +88,12 @@ def tile_encoderrnn_kernel(tc, x, w_emb, b_emb, w_ih_words, w_ih_scales, b_ih, b
         ident_f32 = keep.tile([P, P], F32)
         make_identity(nc, ident_f32[:])
 
+        ones = keep.tile([P, P], BF16)
+        nc.gpsimd.memset(ones[:], 1.0)
+        bias_diag = keep.tile([P, PACK, P], BF16)
+        for t in range(PACK):
+            nc.vector.tensor_scalar_mul(out=bias_diag[:, t, :], in0=ident_bf[:], scalar1=b_emb_sb[:, t : t + 1])
+
         nc.scalar.activation(out=warm[:], in_=warm[:], func=ACT.Sigmoid)
 
         w_t_ps = psum.tile([P, PACK, P], BF16, tag="bank")
@@ -95,11 +104,14 @@ def tile_encoderrnn_kernel(tc, x, w_emb, b_emb, w_ih_words, w_ih_scales, b_ih, b
 
         x_t = keep.tile([P, GROUPS, P], BF16)
 
-        def transpose_x(b):
+        def transpose_x(b, on_scalar):
             x_t_ps = psum.tile([P, PER_BATCH, P], BF16, tag="bank")
             for turn in range(PER_BATCH):
                 nc.tensor.transpose(x_t_ps[:, turn, :], x_sb[:, b, n_of(turn), :], ident_bf[:])
-            nc.scalar.copy(out=x_t[:, b * PER_BATCH : (b + 1) * PER_BATCH, :], in_=x_t_ps[:])
+            if on_scalar:
+                nc.scalar.copy(out=x_t[:, b * PER_BATCH : (b + 1) * PER_BATCH, :], in_=x_t_ps[:])
+            else:
+                nc.vector.tensor_copy(out=x_t[:, b * PER_BATCH : (b + 1) * PER_BATCH, :], in_=x_t_ps[:])
 
         grouped = keep.tile([P, GROUPS, P, PACK], BF16, align_bytes=64)
         emb_codes = keep.tile([P, GROUPS * P], U32, align_bytes=64)
@@ -107,6 +119,12 @@ def tile_encoderrnn_kernel(tc, x, w_emb, b_emb, w_ih_words, w_ih_scales, b_ih, b
 
         def embed_group(g):
             emb_ps = psum.tile([P, PACK, P], F32, tag="bank")
+            if g in SCALAR_EMBEDS:
+                for t in range(PACK):
+                    nc.tensor.matmul(emb_ps[:, t, :], lhsT=w_t[:, t, :], rhs=x_t[:, g, :], start=True, stop=False)
+                    nc.tensor.matmul(emb_ps[:, t, :], lhsT=bias_diag[:, t, :], rhs=ones[:], start=False, stop=True)
+                nc.scalar.copy(out=grouped[:, g], in_=emb_ps[:].rearrange("p t s -> p s t"))
+                return
             for t in range(PACK):
                 nc.tensor.matmul(emb_ps[:, t, :], lhsT=w_t[:, t, :], rhs=x_t[:, g, :], start=True, stop=True)
             nc.vector.tensor_tensor(
@@ -130,11 +148,11 @@ def tile_encoderrnn_kernel(tc, x, w_emb, b_emb, w_ih_words, w_ih_scales, b_ih, b
                 if g == CHUNK_FIRST[c] + CHUNK_GROUPS[c] - 1:
                     quantise_chunk(c)
 
-        transpose_x(0)
-        for g in range(CHUNK_GROUPS[0]):
+        transpose_x(0, on_scalar=True)
+        transpose_x(1, on_scalar=False)
+        transpose_x(2, on_scalar=True)
+        for g in range(EMBEDS_AHEAD):
             embed_and_quantise(g)
-        for b in range(1, BATCH):
-            transpose_x(b)
 
         bias_ps = psum.tile([P, P], BF16, tag="bank")
         nc.tensor.transpose(bias_ps[:], bias_rows[:], ident_bf[:])
@@ -230,8 +248,8 @@ def tile_encoderrnn_kernel(tc, x, w_emb, b_emb, w_ih_words, w_ih_scales, b_ih, b
         n_steps = len(CHUNK_GROUPS) * TILES
         last = len(CHUNK_GROUPS) - 1
         for step in range(n_steps):
-            if CHUNK_GROUPS[0] + step < GROUPS:
-                embed_and_quantise(CHUNK_GROUPS[0] + step)
+            if EMBEDS_AHEAD + step < GROUPS:
+                embed_and_quantise(EMBEDS_AHEAD + step)
             gates(step // TILES, step % TILES)
             if step >= 1:
                 finish((step - 1) // TILES, (step - 1) % TILES, nc.gpsimd)

@@ -142,11 +142,14 @@ def tile_encoderrnn_kernel(tc, x, w_emb, b_emb, w_ih_words, w_ih_scales, b_ih, b
                 in_=grouped[:, first : first + count].rearrange("p g s t -> p (g s t)"),
             )
 
-        def embed_and_quantise(g):
-            embed_group(g)
+        def quantise_behind(g):
             for c in range(len(CHUNK_GROUPS)):
                 if g == CHUNK_FIRST[c] + CHUNK_GROUPS[c] - 1:
                     quantise_chunk(c)
+
+        def embed_and_quantise(g):
+            embed_group(g)
+            quantise_behind(g)
 
         transpose_x(0, on_scalar=True)
         transpose_x(1, on_scalar=False)
@@ -249,8 +252,10 @@ def tile_encoderrnn_kernel(tc, x, w_emb, b_emb, w_ih_words, w_ih_scales, b_ih, b
         last = len(CHUNK_GROUPS) - 1
         for step in range(n_steps):
             if EMBEDS_AHEAD + step < GROUPS:
-                embed_and_quantise(EMBEDS_AHEAD + step)
+                embed_group(EMBEDS_AHEAD + step)
             gates(step // TILES, step % TILES)
+            if EMBEDS_AHEAD + step < GROUPS:
+                quantise_behind(EMBEDS_AHEAD + step)
             if step >= 1:
                 finish((step - 1) // TILES, (step - 1) % TILES, nc.gpsimd)
             if step >= EMIT_LAG:

@@ -248,6 +248,39 @@ def tile_encoderrnn_kernel(tc, x, w_emb, b_emb, w_ih_words, w_ih_scales, b_ih, b
                 transpose_back(h_ps, g, j)
             store_group(h_ps, g, 0, TILES, on_scalar)
 
+        out_sb = keep.tile([P, GROUPS, HID], F32)
+
+        def store_rows(g, cols):
+            b, n = batch_of(g), n_of(g)
+            if n < PER_BATCH - 1:
+                nc.sync.dma_start(out=out_0[b, n : STEPS - 1 : PER_BATCH, cols], in_=out_sb[:, g, cols])
+            else:
+                for first, count in RAGGED_PIECES:
+                    nc.sync.dma_start(
+                        out=out_0[b, PER_BATCH * first + n : PER_BATCH * (first + count) : PER_BATCH, cols],
+                        in_=out_sb[first : first + count, g, cols],
+                    )
+                nc.sync.dma_start(out=out_1[0, b : b + 1, cols], in_=out_sb[P - 1 : P, g, cols])
+
+        def way_out(step, on_scalar):
+            c, j = step // TILES, step % TILES
+            first, count = CHUNK_FIRST[c], CHUNK_GROUPS[c]
+            h_ps = psum.tile([P, count, P], F32, tag="bank")
+            for i in range(count):
+                nc.tensor.transpose(h_ps[:, i, :], h_t[:, j, (first + i) * P : (first + i + 1) * P], ident_f32[:])
+            if on_scalar:
+                nc.scalar.copy(out=out_sb[:, first : first + count, j * P : (j + 1) * P], in_=h_ps[:])
+            else:
+                nc.vector.tensor_copy(out=out_sb[:, first : first + count, j * P : (j + 1) * P], in_=h_ps[:])
+            is_last = c == len(CHUNK_GROUPS) - 1
+            for g in range(first, first + count):
+                if is_last and j == TILES - 2:
+                    store_rows(g, slice(0, (TILES - 1) * P))
+                if is_last and j == TILES - 1:
+                    store_rows(g, slice((TILES - 1) * P, HID))
+                if not is_last and j == TILES - 1:
+                    store_rows(g, slice(0, HID))
+
         n_steps = len(CHUNK_GROUPS) * TILES
         last = len(CHUNK_GROUPS) - 1
         for step in range(n_steps):
@@ -258,20 +291,9 @@ def tile_encoderrnn_kernel(tc, x, w_emb, b_emb, w_ih_words, w_ih_scales, b_ih, b
                 quantise_behind(EMBEDS_AHEAD + step)
             if step >= 1:
                 finish((step - 1) // TILES, (step - 1) % TILES, nc.gpsimd)
-            if step >= EMIT_LAG:
-                emit(step - EMIT_LAG, on_scalar=False)
+            if step >= 4:
+                way_out(step - 4, on_scalar=False)
 
         finish(last, TILES - 1, nc.vector)
-        for g in range(n_steps - EMIT_LAG, CHUNK_FIRST[last]):
-            emit(g, on_scalar=(g % 2 == 1))
-        last_groups = range(CHUNK_FIRST[last], GROUPS)
-        last_ps = {}
-        for g in last_groups:
-            h_ps = psum.tile([P, HID], F32, tag="bank")
-            last_ps[g] = h_ps
-            for j in range(TILES - 1):
-                transpose_back(h_ps, g, j)
-            store_group(h_ps, g, 0, TILES - 1, on_scalar=(g % 2 == 1))
-        for g in last_groups:
-            transpose_back(last_ps[g], g, TILES - 1)
-            store_group(last_ps[g], g, TILES - 1, 1, on_scalar=(g % 2 == 1))
+        for step in range(n_steps - 4, n_steps):
+            way_out(step, on_scalar=(step % 2 == 1))

@@ -278,8 +278,10 @@ def tile_encoderrnn_kernel(tc, x, w_emb, b_emb, w_ih_words, w_ih_scales, b_ih, b
                     store_rows(g, slice(0, (TILES - 1) * P))
                 if is_last and j == TILES - 1:
                     store_rows(g, slice((TILES - 1) * P, HID))
+                if not is_last and j == TILES // 2 - 1:
+                    store_rows(g, slice(0, HID // 2))
                 if not is_last and j == TILES - 1:
-                    store_rows(g, slice(0, HID))
+                    store_rows(g, slice(HID // 2, HID))
 
         n_steps = len(CHUNK_GROUPS) * TILES
         last = len(CHUNK_GROUPS) - 1
@@ -291,9 +293,10 @@ def tile_encoderrnn_kernel(tc, x, w_emb, b_emb, w_ih_words, w_ih_scales, b_ih, b
                 quantise_behind(EMBEDS_AHEAD + step)
             if step >= 1:
                 finish((step - 1) // TILES, (step - 1) % TILES, nc.gpsimd)
-            if step >= 4:
+            if step >= 4 and (step - 4) % 2 == 1:
+                way_out(step - 4 - 1, on_scalar=False)
                 way_out(step - 4, on_scalar=False)
 
         finish(last, TILES - 1, nc.vector)
-        for step in range(n_steps - 4, n_steps):
+        for step in range(2 * ((n_steps - 4) // 2), n_steps):
             way_out(step, on_scalar=(step % 2 == 1))

@@ -41,6 +41,15 @@ FLOPS = 2 * BATCH * STEPS * IN * HID + 2 * BATCH * STEPS * HID * 3 * HID
 RAGGED_PIECES = ((0, 64), (64, 32), (96, 16), (112, 15))
 
 
+def embed_in_step(step):
+    complete = CHUNK_FIRST[2] - EMBEDS_AHEAD
+    if step < complete:
+        return EMBEDS_AHEAD + step
+    if step == complete:
+        return GROUPS
+    return EMBEDS_AHEAD + step - 1
+
+
 def batch_of(g):
     return g // PER_BATCH
 
@@ -286,11 +295,12 @@ def tile_encoderrnn_kernel(tc, x, w_emb, b_emb, w_ih_words, w_ih_scales, b_ih, b
         n_steps = len(CHUNK_GROUPS) * TILES
         last = len(CHUNK_GROUPS) - 1
         for step in range(n_steps):
-            if EMBEDS_AHEAD + step < GROUPS:
-                embed_group(EMBEDS_AHEAD + step)
+            embedded = embed_in_step(step)
+            if embedded < GROUPS:
+                embed_group(embedded)
             gates(step // TILES, step % TILES)
-            if EMBEDS_AHEAD + step < GROUPS:
-                quantise_behind(EMBEDS_AHEAD + step)
+            if embedded < GROUPS:
+                quantise_behind(embedded)
             if step >= 1:
                 finish((step - 1) // TILES, (step - 1) % TILES, nc.gpsimd)
             if step >= 4 and (step - 4) % 2 == 1:

@@ -35,6 +35,7 @@ EMIT_LAG = 7
 
 SCALAR_EMBEDS = (1, 3)
 EMBEDS_AHEAD = 4
+WARM_MATMULS = 10
 
 FLOPS = 2 * BATCH * STEPS * IN * HID + 2 * BATCH * STEPS * HID * 3 * HID
 
@@ -74,6 +75,11 @@ def tile_encoderrnn_kernel(tc, x, w_emb, b_emb, w_ih_words, w_ih_scales, b_ih, b
         bias_rows = keep.tile([P, P], BF16)
         warm = keep.tile([P, 1], F32)
 
+        zeros = keep.tile([P, P], BF16)
+        nc.vector.memset(zeros[:], 0.0)
+        dummy_ps = psum.tile([P, PACK, P], F32, tag="bank")
+        for i in range(WARM_MATMULS):
+            nc.tensor.matmul(dummy_ps[:, i % PACK, :], lhsT=zeros[:], rhs=zeros[:], start=True, stop=True)
         nc.vector.memset(w_plane[:].bitcast(I32), 0)
         nc.vector.memset(bias_rows[:], 0.0)
         nc.vector.memset(warm[:], 0.0)

@@ -51,12 +51,23 @@ def embed_in_step(step):
     return EMBEDS_AHEAD + step - 1
 
 
+def order_of_groups():
+    order = [(0, 3), (0, 0), (0, 1), (0, 2), (1, 3), (2, 3)]
+    for b in range(1, BATCH):
+        for n in range(PER_BATCH - 1):
+            order.append((b, n))
+    return order
+
+
+ORDER = order_of_groups()
+
+
 def batch_of(g):
-    return g // PER_BATCH
+    return ORDER[g][0]
 
 
 def n_of(g):
-    return (g + PER_BATCH - 1) % PER_BATCH
+    return ORDER[g][1]
 
 
 def tile_encoderrnn_kernel(tc, x, w_emb, b_emb, w_ih_words, w_ih_scales, b_ih, b_hh, out_0, out_1):
@@ -64,7 +75,6 @@ def tile_encoderrnn_kernel(tc, x, w_emb, b_emb, w_ih_words, w_ih_scales, b_ih, b
     with ExitStack() as stack:
         keep = stack.enter_context(tc.tile_pool(name="keep", bufs=1))
         work = stack.enter_context(tc.tile_pool(name="work", bufs=4))
-        leave = stack.enter_context(tc.tile_pool(name="leave", bufs=6))
         psum = stack.enter_context(tc.psum_pool(name="psum", bufs=8))
 
         x_sb = keep.tile([P, BATCH, PER_BATCH, IN], BF16)
@@ -117,16 +127,16 @@ def tile_encoderrnn_kernel(tc, x, w_emb, b_emb, w_ih_words, w_ih_scales, b_ih, b
         w_t = keep.tile([P, PACK, P], BF16)
         nc.vector.tensor_copy(out=w_t[:], in_=w_t_ps[:])
 
-        x_t = keep.tile([P, GROUPS, P], BF16)
+        x_t = keep.tile([P, BATCH, PER_BATCH, P], BF16)
 
         def transpose_x(b, on_scalar):
             x_t_ps = psum.tile([P, PER_BATCH, P], BF16, tag="bank")
-            for turn in range(PER_BATCH):
-                nc.tensor.transpose(x_t_ps[:, turn, :], x_sb[:, b, n_of(turn), :], ident_bf[:])
+            for n in range(PER_BATCH):
+                nc.tensor.transpose(x_t_ps[:, n, :], x_sb[:, b, n, :], ident_bf[:])
             if on_scalar:
-                nc.scalar.copy(out=x_t[:, b * PER_BATCH : (b + 1) * PER_BATCH, :], in_=x_t_ps[:])
+                nc.scalar.copy(out=x_t[:, b], in_=x_t_ps[:])
             else:
-                nc.vector.tensor_copy(out=x_t[:, b * PER_BATCH : (b + 1) * PER_BATCH, :], in_=x_t_ps[:])
+                nc.vector.tensor_copy(out=x_t[:, b], in_=x_t_ps[:])
 
         grouped = keep.tile([P, GROUPS, P, PACK], BF16, align_bytes=64)
         emb_codes = keep.tile([P, GROUPS * P], U32, align_bytes=64)
@@ -136,12 +146,12 @@ def tile_encoderrnn_kernel(tc, x, w_emb, b_emb, w_ih_words, w_ih_scales, b_ih, b
             emb_ps = psum.tile([P, PACK, P], F32, tag="bank")
             if g in SCALAR_EMBEDS:
                 for t in range(PACK):
-                    nc.tensor.matmul(emb_ps[:, t, :], lhsT=w_t[:, t, :], rhs=x_t[:, g, :], start=True, stop=False)
+                    nc.tensor.matmul(emb_ps[:, t, :], lhsT=w_t[:, t, :], rhs=x_t[:, batch_of(g), n_of(g), :], start=True, stop=False)
                     nc.tensor.matmul(emb_ps[:, t, :], lhsT=bias_diag[:, t, :], rhs=ones[:], start=False, stop=True)
                 nc.scalar.copy(out=grouped[:, g], in_=emb_ps[:].rearrange("p t s -> p s t"))
                 return
             for t in range(PACK):
-                nc.tensor.matmul(emb_ps[:, t, :], lhsT=w_t[:, t, :], rhs=x_t[:, g, :], start=True, stop=True)
+                nc.tensor.matmul(emb_ps[:, t, :], lhsT=w_t[:, t, :], rhs=x_t[:, batch_of(g), n_of(g), :], start=True, stop=True)
             nc.vector.tensor_tensor(
                 out=grouped[:, g],
                 in0=emb_ps[:].rearrange("p t s -> p s t"),
@@ -236,46 +246,37 @@ def tile_encoderrnn_kernel(tc, x, w_emb, b_emb, w_ih_words, w_ih_scales, b_ih, b
             nc.scalar.activation(out=n_sb[:], in_=pre_n[:], func=ACT.Tanh, bias=b_in[:, j : j + 1], scale=1.0)
             product_engine.tensor_mul(out=h_t[:, j, columns_of(c)], in0=one_minus_z[:], in1=n_sb[:])
 
-        def transpose_back(h_ps, g, j):
-            nc.tensor.transpose(h_ps[:, j * P : (j + 1) * P], h_t[:, j, g * P : (g + 1) * P], ident_f32[:])
-
-        def store_group(h_ps, g, first_tile, n_tiles, on_scalar):
-            b, n = batch_of(g), n_of(g)
-            cols = slice(first_tile * P, (first_tile + n_tiles) * P)
-            h_sb = leave.tile([P, n_tiles * P], F32)
-            if on_scalar:
-                nc.scalar.copy(out=h_sb[:], in_=h_ps[:, cols])
-            else:
-                nc.vector.tensor_copy(out=h_sb[:], in_=h_ps[:, cols])
-            if n < PER_BATCH - 1:
-                nc.sync.dma_start(out=out_0[b, n : STEPS - 1 : PER_BATCH, cols], in_=h_sb[:])
-            else:
-                for first, count in RAGGED_PIECES:
-                    nc.sync.dma_start(
-                        out=out_0[b, PER_BATCH * first + n : PER_BATCH * (first + count) : PER_BATCH, cols],
-                        in_=h_sb[first : first + count, :],
-                    )
-                nc.sync.dma_start(out=out_1[0, b : b + 1, cols], in_=h_sb[P - 1 : P, :])
-
-        def emit(g, on_scalar):
-            h_ps = psum.tile([P, HID], F32, tag="bank")
-            for j in range(TILES):
-                transpose_back(h_ps, g, j)
-            store_group(h_ps, g, 0, TILES, on_scalar)
-
         out_sb = keep.tile([P, GROUPS, HID], F32)
+        out_rows = out_0.rearrange("b s h -> (b s) h")
 
-        def store_rows(g, cols):
+        def store_rows(g, count, cols):
             b, n = batch_of(g), n_of(g)
-            if n < PER_BATCH - 1:
-                nc.sync.dma_start(out=out_0[b, n : STEPS - 1 : PER_BATCH, cols], in_=out_sb[:, g, cols])
-            else:
-                for first, count in RAGGED_PIECES:
+            if n == PER_BATCH - 1:
+                for first, rows in RAGGED_PIECES:
                     nc.sync.dma_start(
-                        out=out_0[b, PER_BATCH * first + n : PER_BATCH * (first + count) : PER_BATCH, cols],
-                        in_=out_sb[first : first + count, g, cols],
+                        out=out_0[b, PER_BATCH * first + n : PER_BATCH * (first + rows) : PER_BATCH, cols],
+                        in_=out_sb[first : first + rows, g, cols],
                     )
                 nc.sync.dma_start(out=out_1[0, b : b + 1, cols], in_=out_sb[P - 1 : P, g, cols])
+            elif count == 1:
+                nc.sync.dma_start(out=out_0[b, n : STEPS - 1 : PER_BATCH, cols], in_=out_sb[:, g, cols])
+            else:
+                top = b * (STEPS - 1) + n
+                rows = out_rows[top : top + STEPS].rearrange("(p n) h -> p n h", n=PER_BATCH)
+                nc.sync.dma_start(out=rows[:, 0:count, cols], in_=out_sb[:, g : g + count, cols])
+
+        def store_chunk(c, cols):
+            g, end = CHUNK_FIRST[c], CHUNK_FIRST[c] + CHUNK_GROUPS[c]
+            while g < end:
+                count = 1
+                while (
+                    g + count < end
+                    and batch_of(g) == batch_of(g + count) < BATCH - 1
+                    and n_of(g) + count == n_of(g + count)
+                ):
+                    count += 1
+                store_rows(g, count, cols)
+                g += count
 
         def way_out(step, on_scalar):
             c, j = step // TILES, step % TILES
@@ -287,16 +288,15 @@ def tile_encoderrnn_kernel(tc, x, w_emb, b_emb, w_ih_words, w_ih_scales, b_ih, b
                 nc.scalar.copy(out=out_sb[:, first : first + count, j * P : (j + 1) * P], in_=h_ps[:])
             else:
                 nc.vector.tensor_copy(out=out_sb[:, first : first + count, j * P : (j + 1) * P], in_=h_ps[:])
-            is_last = c == len(CHUNK_GROUPS) - 1
-            for g in range(first, first + count):
-                if is_last and j == TILES - 2:
-                    store_rows(g, slice(0, (TILES - 1) * P))
-                if is_last and j == TILES - 1:
-                    store_rows(g, slice((TILES - 1) * P, HID))
-                if not is_last and j == TILES // 2 - 1:
-                    store_rows(g, slice(0, HID // 2))
-                if not is_last and j == TILES - 1:
-                    store_rows(g, slice(HID // 2, HID))
+            if c == len(CHUNK_GROUPS) - 1:
+                if j == TILES - 2:
+                    store_chunk(c, slice(0, (TILES - 1) * P))
+                if j == TILES - 1:
+                    store_chunk(c, slice((TILES - 1) * P, HID))
+            elif j == TILES // 2 - 1:
+                store_chunk(c, slice(0, HID // 2))
+            elif j == TILES - 1:
+                store_chunk(c, slice(HID // 2, HID))
 
         n_steps = len(CHUNK_GROUPS) * TILES
         last = len(CHUNK_GROUPS) - 1

@@ -37,6 +37,13 @@ SCALAR_EMBEDS = (1, 3)
 EMBEDS_AHEAD = 4
 WARM_MATMULS = 10
 
+ROWS = 4
+SUM = 0
+MINUS_SUM = 1
+B_IH = 2
+B_HH = 3
+PER_ROW = GATE_TILES // ROWS
+
 FLOPS = 2 * BATCH * STEPS * IN * HID + 2 * BATCH * STEPS * HID * 3 * HID
 
 RAGGED_PIECES = ((0, 64), (64, 32), (96, 16), (112, 15))
@@ -82,7 +89,7 @@ def tile_encoderrnn_kernel(tc, x, w_emb, b_emb, w_ih_words, w_ih_scales, b_ih, b
         b_emb_sb = keep.tile([P, PACK], BF16)
         w_words = keep.tile([P, 2 * 3 * HID], U8, align_bytes=64)
         w_plane = keep.tile([P, 3 * HID], U8, align_bytes=64)
-        bias_rows = keep.tile([P, P], BF16)
+        bias_rows = keep.tile([P, PER_ROW * P], BF16)
         warm = keep.tile([P, 1], F32)
 
         zeros = keep.tile([P, P], BF16)
@@ -105,14 +112,18 @@ def tile_encoderrnn_kernel(tc, x, w_emb, b_emb, w_ih_words, w_ih_scales, b_ih, b
                 out=w_plane[32 * quadrant : 32 * quadrant + 4, :].bitcast(I32),
                 in_=w_ih_scales[0, 4 * quadrant : 4 * quadrant + 4, :].bitcast(I32),
             )
-        nc.sync.dma_start(out=bias_rows[0:GATE_TILES, :], in_=b_ih.rearrange("(m q) -> m q", q=P))
-        nc.sync.dma_start(out=bias_rows[GATE_TILES : 2 * GATE_TILES, :], in_=b_hh.rearrange("(m q) -> m q", q=P))
+        nc.sync.dma_start(out=bias_rows[0:ROWS, :], in_=b_ih.rearrange("(a c) -> a c", a=ROWS))
+        nc.sync.dma_start(out=bias_rows[ROWS : 2 * ROWS, :], in_=b_hh.rearrange("(a c) -> a c", a=ROWS))
 
         ident_bf = keep.tile([P, P], BF16)
         make_identity(nc, ident_bf[:])
         ident_f32 = keep.tile([P, P], F32)
         make_identity(nc, ident_f32[:])
 
+        pick = keep.tile([P, 4, ROWS], BF16)
+        nc.vector.tensor_add(out=pick[:, SUM, :], in0=ident_bf[:, 0:ROWS], in1=ident_bf[:, ROWS : 2 * ROWS])
+        nc.vector.tensor_scalar_mul(out=pick[:, MINUS_SUM, :], in0=pick[:, SUM, :], scalar1=-1.0)
+        nc.vector.tensor_copy(out=pick[:, B_IH : B_HH + 1, :], in_=ident_bf[:, 0 : 2 * ROWS].rearrange("p (k a) -> p k a", k=2))
         ones = keep.tile([P, P], BF16)
         nc.gpsimd.memset(ones[:], 1.0)
         bias_diag = keep.tile([P, PACK, P], BF16)
@@ -176,32 +187,29 @@ def tile_encoderrnn_kernel(tc, x, w_emb, b_emb, w_ih_words, w_ih_scales, b_ih, b
             embed_group(g)
             quantise_behind(g)
 
+        bias_cols = keep.tile([P, PER_ROW, 4 * ROWS], F32)
+
+        def gate_biases():
+            bias_ps = psum.tile([P, PER_ROW, 4 * ROWS], F32, tag="bank")
+            for k in range(PER_ROW):
+                nc.tensor.matmul(
+                    bias_ps[:, k, :], lhsT=bias_rows[:, k * P : (k + 1) * P], rhs=pick[:].rearrange("p k a -> p (k a)"), start=True, stop=True
+                )
+            nc.scalar.copy(out=bias_cols[:], in_=bias_ps[:])
+
+        def bias_col(kind, gate, j):
+            m = gate * TILES + j
+            column = kind * ROWS + m // PER_ROW
+            return bias_cols[:, m % PER_ROW, column : column + 1]
+
         transpose_x(0, on_scalar=True)
         transpose_x(1, on_scalar=False)
         transpose_x(2, on_scalar=True)
         for g in range(EMBEDS_AHEAD):
+            if g == SCALAR_EMBEDS[-1]:
+                gate_biases()
             embed_and_quantise(g)
 
-        bias_ps = psum.tile([P, P], BF16, tag="bank")
-        nc.tensor.transpose(bias_ps[:], bias_rows[:], ident_bf[:])
-        bias_cols = keep.tile([P, 2 * GATE_TILES], F32)
-        nc.scalar.copy(out=bias_cols[:], in_=bias_ps[:, 0 : 2 * GATE_TILES])
-        minus_cols = keep.tile([P, 2 * GATE_TILES], F32)
-        nc.scalar.mul(out=minus_cols[:], in_=bias_ps[:, 0 : 2 * GATE_TILES], mul=-1.0)
-        b_in = bias_cols[:, N * TILES : (N + 1) * TILES]
-        b_hn = bias_cols[:, GATE_TILES + N * TILES : GATE_TILES + (N + 1) * TILES]
-        b_r = keep.tile([P, TILES], F32)
-        nc.gpsimd.tensor_add(
-            out=b_r[:],
-            in0=bias_cols[:, R * TILES : (R + 1) * TILES],
-            in1=bias_cols[:, GATE_TILES + R * TILES : GATE_TILES + (R + 1) * TILES],
-        )
-        minus_b_z = keep.tile([P, TILES], F32)
-        nc.gpsimd.tensor_add(
-            out=minus_b_z[:],
-            in0=minus_cols[:, Z * TILES : (Z + 1) * TILES],
-            in1=minus_cols[:, GATE_TILES + Z * TILES : GATE_TILES + (Z + 1) * TILES],
-        )
 
         def columns_of(c):
             return slice(CHUNK_FIRST[c] * P, (CHUNK_FIRST[c] + CHUNK_GROUPS[c]) * P)
@@ -229,21 +237,21 @@ def tile_encoderrnn_kernel(tc, x, w_emb, b_emb, w_ih_words, w_ih_scales, b_ih, b
             z_ps = gate_pass(c, Z, j)
             n_ps = gate_pass(c, N, j)
             r_sb = work.tile([P, width], F32)
-            nc.scalar.activation(out=r_sb[:], in_=r_ps[:], func=ACT.Sigmoid, bias=b_r[:, j : j + 1], scale=1.0)
+            nc.scalar.activation(out=r_sb[:], in_=r_ps[:], func=ACT.Sigmoid, bias=bias_col(SUM, R, j), scale=1.0)
             one_minus_z = work.tile([P, width], F32)
             nc.scalar.activation(
-                out=one_minus_z[:], in_=z_ps[:], func=ACT.Sigmoid, bias=minus_b_z[:, j : j + 1], scale=-1.0
+                out=one_minus_z[:], in_=z_ps[:], func=ACT.Sigmoid, bias=bias_col(MINUS_SUM, Z, j), scale=-1.0
             )
             pre_n = work.tile([P, width], F32)
             nc.vector.scalar_tensor_tensor(
-                out=pre_n[:], in0=r_sb[:], scalar=b_hn[:, j : j + 1], in1=n_ps[:], op0=ALU.mult, op1=ALU.add
+                out=pre_n[:], in0=r_sb[:], scalar=bias_col(B_HH, N, j), in1=n_ps[:], op0=ALU.mult, op1=ALU.add
             )
             halves_of[(c, j)] = (one_minus_z, pre_n)
 
         def finish(c, j, product_engine):
             one_minus_z, pre_n = halves_of[(c, j)]
             n_sb = work.tile([P, CHUNK_GROUPS[c] * P], F32)
-            nc.scalar.activation(out=n_sb[:], in_=pre_n[:], func=ACT.Tanh, bias=b_in[:, j : j + 1], scale=1.0)
+            nc.scalar.activation(out=n_sb[:], in_=pre_n[:], func=ACT.Tanh, bias=bias_col(B_IH, N, j), scale=1.0)
             product_engine.tensor_mul(out=h_t[:, j, columns_of(c)], in0=one_minus_z[:], in1=n_sb[:])
 
         out_sb = keep.tile([P, GROUPS, HID], F32)

@@ -33,7 +33,7 @@ assert sum(CHUNK_GROUPS) == GROUPS
 
 EMIT_LAG = 7
 
-SCALAR_EMBEDS = (1, 3)
+SCALAR_EMBEDS = (2,)
 EMBEDS_AHEAD = 4
 WARM_MATMULS = 10
 
@@ -46,7 +46,7 @@ PER_ROW = GATE_TILES // ROWS
 
 FLOPS = 2 * BATCH * STEPS * IN * HID + 2 * BATCH * STEPS * HID * 3 * HID
 
-RAGGED_PIECES = ((0, 64), (64, 32), (96, 16), (112, 15))
+RAGGED_PIECES = ((0, 64), (64, 63))
 
 
 def embed_in_step(step):
@@ -101,8 +101,8 @@ def tile_encoderrnn_kernel(tc, x, w_emb, b_emb, w_ih_words, w_ih_scales, b_ih, b
         nc.vector.memset(bias_rows[:], 0.0)
         nc.vector.memset(warm[:], 0.0)
 
-        nc.sync.dma_start(out=x_sb[:, 0], in_=x[0].rearrange("(p n) i -> p n i", n=PER_BATCH))
-        nc.scalar.dma_start(out=w_sb[:], in_=w_emb.rearrange("(p t) i -> p t i", t=PACK))
+        nc.sync.dma_start(out=w_sb[:], in_=w_emb.rearrange("(p t) i -> p t i", t=PACK))
+        nc.scalar.dma_start(out=x_sb[:, 0], in_=x[0].rearrange("(p n) i -> p n i", n=PER_BATCH))
         nc.sync.dma_start(out=b_emb_sb[:], in_=b_emb.rearrange("(p t) -> p t", t=PACK))
         for b in range(1, BATCH):
             nc.scalar.dma_start(out=x_sb[:, b], in_=x[b].rearrange("(p n) i -> p n i", n=PER_BATCH))
@@ -206,7 +206,7 @@ def tile_encoderrnn_kernel(tc, x, w_emb, b_emb, w_ih_words, w_ih_scales, b_ih, b
         transpose_x(1, on_scalar=False)
         transpose_x(2, on_scalar=True)
         for g in range(EMBEDS_AHEAD):
-            if g == SCALAR_EMBEDS[-1]:
+            if g == 3:
                 gate_biases()
             embed_and_quantise(g)
 
@@ -248,11 +248,19 @@ def tile_encoderrnn_kernel(tc, x, w_emb, b_emb, w_ih_words, w_ih_scales, b_ih, b
             )
             halves_of[(c, j)] = (one_minus_z, pre_n)
 
-        def finish(c, j, product_engine):
-            one_minus_z, pre_n = halves_of[(c, j)]
+        n_of_step = {}
+
+        def tanh(step):
+            c, j = step // TILES, step % TILES
             n_sb = work.tile([P, CHUNK_GROUPS[c] * P], F32)
-            nc.scalar.activation(out=n_sb[:], in_=pre_n[:], func=ACT.Tanh, bias=bias_col(B_IH, N, j), scale=1.0)
-            product_engine.tensor_mul(out=h_t[:, j, columns_of(c)], in0=one_minus_z[:], in1=n_sb[:])
+            nc.scalar.activation(
+                out=n_sb[:], in_=halves_of[(c, j)][1][:], func=ACT.Tanh, bias=bias_col(B_IH, N, j), scale=1.0
+            )
+            n_of_step[step] = n_sb
+
+        def product(step, engine):
+            c, j = step // TILES, step % TILES
+            engine.tensor_mul(out=h_t[:, j, columns_of(c)], in0=halves_of[(c, j)][0][:], in1=n_of_step[step][:])
 
         out_sb = keep.tile([P, GROUPS, HID], F32)
         out_rows = out_0.rearrange("b s h -> (b s) h")
@@ -260,18 +268,24 @@ def tile_encoderrnn_kernel(tc, x, w_emb, b_emb, w_ih_words, w_ih_scales, b_ih, b
         def store_rows(g, count, cols):
             b, n = batch_of(g), n_of(g)
             if n == PER_BATCH - 1:
-                for first, rows in RAGGED_PIECES:
-                    nc.sync.dma_start(
-                        out=out_0[b, PER_BATCH * first + n : PER_BATCH * (first + rows) : PER_BATCH, cols],
-                        in_=out_sb[first : first + rows, g, cols],
-                    )
+                if b < BATCH - 1:
+                    top = b * (STEPS - 1)
+                    rows = out_rows[top : top + STEPS].rearrange("(p n) h -> p n h", n=PER_BATCH)
+                    nc.sync.dma_start(out=rows[:, n, cols], in_=out_sb[:, g, cols])
+                else:
+                    for first, count_p in RAGGED_PIECES:
+                        nc.sync.dma_start(
+                            out=out_0[b, PER_BATCH * first + n : PER_BATCH * (first + count_p) : PER_BATCH, cols],
+                            in_=out_sb[first : first + count_p, g, cols],
+                        )
                 nc.sync.dma_start(out=out_1[0, b : b + 1, cols], in_=out_sb[P - 1 : P, g, cols])
             elif count == 1:
                 nc.sync.dma_start(out=out_0[b, n : STEPS - 1 : PER_BATCH, cols], in_=out_sb[:, g, cols])
             else:
-                top = b * (STEPS - 1) + n
+                back = 1 if b == BATCH - 1 else 0
+                top = b * (STEPS - 1) - back
                 rows = out_rows[top : top + STEPS].rearrange("(p n) h -> p n h", n=PER_BATCH)
-                nc.sync.dma_start(out=rows[:, 0:count, cols], in_=out_sb[:, g : g + count, cols])
+                nc.sync.dma_start(out=rows[:, n + back : n + back + count, cols], in_=out_sb[:, g : g + count, cols])
 
         def store_chunk(c, cols):
             g, end = CHUNK_FIRST[c], CHUNK_FIRST[c] + CHUNK_GROUPS[c]
@@ -279,8 +293,8 @@ def tile_encoderrnn_kernel(tc, x, w_emb, b_emb, w_ih_words, w_ih_scales, b_ih, b
                 count = 1
                 while (
                     g + count < end
-                    and batch_of(g) == batch_of(g + count) < BATCH - 1
-                    and n_of(g) + count == n_of(g + count)
+                    and batch_of(g) == batch_of(g + count)
+                    and n_of(g) + count == n_of(g + count) < PER_BATCH - 1
                 ):
                     count += 1
                 store_rows(g, count, cols)
@@ -296,13 +310,10 @@ def tile_encoderrnn_kernel(tc, x, w_emb, b_emb, w_ih_words, w_ih_scales, b_ih, b
                 nc.scalar.copy(out=out_sb[:, first : first + count, j * P : (j + 1) * P], in_=h_ps[:])
             else:
                 nc.vector.tensor_copy(out=out_sb[:, first : first + count, j * P : (j + 1) * P], in_=h_ps[:])
-            if c == len(CHUNK_GROUPS) - 1:
-                if j == TILES - 2:
-                    store_chunk(c, slice(0, (TILES - 1) * P))
-                if j == TILES - 1:
-                    store_chunk(c, slice((TILES - 1) * P, HID))
-            elif j == TILES // 2 - 1:
+            if j == TILES // 2 - 1:
                 store_chunk(c, slice(0, HID // 2))
+            elif j >= TILES // 2 and c >= len(CHUNK_GROUPS) - 2:
+                store_chunk(c, slice(j * P, (j + 1) * P))
             elif j == TILES - 1:
                 store_chunk(c, slice(HID // 2, HID))
 
@@ -316,11 +327,17 @@ def tile_encoderrnn_kernel(tc, x, w_emb, b_emb, w_ih_words, w_ih_scales, b_ih, b
             if embedded < GROUPS:
                 quantise_behind(embedded)
             if step >= 1:
-                finish((step - 1) // TILES, (step - 1) % TILES, nc.gpsimd)
-            if step >= 4 and (step - 4) % 2 == 1:
+                tanh(step - 1)
+                if step < n_steps - 1:
+                    product(step - 1, nc.gpsimd)
+            if step >= 4 and (step - 4) % 2 == 1 and step < n_steps - 1:
                 way_out(step - 4 - 1, on_scalar=False)
                 way_out(step - 4, on_scalar=False)
 
-        finish(last, TILES - 1, nc.vector)
-        for step in range(2 * ((n_steps - 4) // 2), n_steps):
+        way_out(n_steps - 6, on_scalar=False)
+        product(n_steps - 2, nc.vector)
+        tanh(n_steps - 1)
+        way_out(n_steps - 5, on_scalar=True)
+        product(n_steps - 1, nc.vector)
+        for step in range(n_steps - 4, n_steps):
             way_out(step, on_scalar=(step % 2 == 1))

@@ -170,13 +170,21 @@ def tile_encoderrnn_kernel(tc, x, w_emb, b_emb, w_ih_words, w_ih_scales, b_ih, b
                 op=ALU.add,
             )
 
-        def quantise_chunk(c):
-            first, count = CHUNK_FIRST[c], CHUNK_GROUPS[c]
+        def quantise_groups(first, count):
+            cols = slice(first * P, (first + count) * P)
             nc.vector.quantize_mx(
-                out=emb_codes[:, first * P : (first + count) * P].bitcast(FP8X4),
-                scales=emb_plane[:, first * P : (first + count) * P],
+                out=emb_codes[:, cols].bitcast(FP8X4),
+                scales=emb_plane[:, cols],
                 in_=grouped[:, first : first + count].rearrange("p g s t -> p (g s t)"),
             )
+
+        def quantise_chunk(c):
+            first, count = CHUNK_FIRST[c], CHUNK_GROUPS[c]
+            if c > 0:
+                quantise_groups(first, count)
+                return
+            for g in range(first, first + count):
+                quantise_groups(g, 1)
 
         def quantise_behind(g):
             for c in range(len(CHUNK_GROUPS)):

from contextlib import ExitStack

import concourse.mybir as mybir
from concourse.masks import make_identity

BF16 = mybir.dt.bfloat16
F32 = mybir.dt.float32
I32 = mybir.dt.int32
U32 = mybir.dt.uint32
U8 = mybir.dt.uint8
FP8X4 = mybir.dt.float8_e4m3fn_x4
FP4X4 = mybir.dt.float4_e2m1fn_x4
ACT = mybir.ActivationFunctionType
ALU = mybir.AluOpType

P = 128
PACK = 4
BATCH = 3
STEPS = 512
IN = 128
HID = 512
PER_BATCH = STEPS // P
GROUPS = BATCH * PER_BATCH
TILES = HID // P
GATE_TILES = 3 * TILES
R = 0
Z = 1
N = 2

CHUNK_GROUPS = (2, 4, 4, 2)
CHUNK_FIRST = (0, 2, 6, 10)
assert sum(CHUNK_GROUPS) == GROUPS

EMIT_LAG = 7

SCALAR_EMBEDS = (2,)
EMBEDS_AHEAD = 4
WARM_MATMULS = 10

ROWS = 4
SUM = 0
MINUS_SUM = 1
B_IH = 2
B_HH = 3
PER_ROW = GATE_TILES // ROWS

FLOPS = 2 * BATCH * STEPS * IN * HID + 2 * BATCH * STEPS * HID * 3 * HID

RAGGED_PIECES = ((0, 64), (64, 63))


def embed_in_step(step):
    complete = CHUNK_FIRST[2] - EMBEDS_AHEAD
    if step < complete:
        return EMBEDS_AHEAD + step
    if step == complete:
        return GROUPS
    return EMBEDS_AHEAD + step - 1


def order_of_groups():
    order = [(0, 3), (0, 0), (0, 1), (0, 2), (1, 3), (2, 3)]
    for b in range(1, BATCH):
        for n in range(PER_BATCH - 1):
            order.append((b, n))
    return order


ORDER = order_of_groups()


def batch_of(g):
    return ORDER[g][0]


def n_of(g):
    return ORDER[g][1]


def tile_encoderrnn_kernel(tc, x, w_emb, b_emb, w_ih_words, w_ih_scales, b_ih, b_hh, out_0, out_1):
    nc = tc.nc
    with ExitStack() as stack:
        keep = stack.enter_context(tc.tile_pool(name="keep", bufs=1))
        work = stack.enter_context(tc.tile_pool(name="work", bufs=4))
        psum = stack.enter_context(tc.psum_pool(name="psum", bufs=8))

        x_sb = keep.tile([P, BATCH, PER_BATCH, IN], BF16)
        w_sb = keep.tile([P, PACK, IN], BF16)
        b_emb_sb = keep.tile([P, PACK], BF16)
        w_words = keep.tile([P, 2 * 3 * HID], U8, align_bytes=64)
        w_plane = keep.tile([P, 3 * HID], U8, align_bytes=64)
        bias_rows = keep.tile([P, PER_ROW * P], BF16)
        warm = keep.tile([P, 1], F32)

        zeros = keep.tile([P, P], BF16)
        nc.vector.memset(zeros[:], 0.0)
        dummy_ps = psum.tile([P, PACK, P], F32, tag="bank")
        for i in range(WARM_MATMULS):
            nc.tensor.matmul(dummy_ps[:, i % PACK, :], lhsT=zeros[:], rhs=zeros[:], start=True, stop=True)
        nc.vector.memset(w_plane[:].bitcast(I32), 0)
        nc.vector.memset(bias_rows[:], 0.0)
        nc.vector.memset(warm[:], 0.0)

        nc.sync.dma_start(out=w_sb[:], in_=w_emb.rearrange("(p t) i -> p t i", t=PACK))
        nc.scalar.dma_start(out=x_sb[:, 0], in_=x[0].rearrange("(p n) i -> p n i", n=PER_BATCH))
        nc.sync.dma_start(out=b_emb_sb[:], in_=b_emb.rearrange("(p t) -> p t", t=PACK))
        for b in range(1, BATCH):
            nc.scalar.dma_start(out=x_sb[:, b], in_=x[b].rearrange("(p n) i -> p n i", n=PER_BATCH))
        nc.sync.dma_start(out=w_words[:].bitcast(I32), in_=w_ih_words[0].bitcast(I32))
        for quadrant in range(4):
            nc.sync.dma_start(
                out=w_plane[32 * quadrant : 32 * quadrant + 4, :].bitcast(I32),
                in_=w_ih_scales[0, 4 * quadrant : 4 * quadrant + 4, :].bitcast(I32),
            )
        nc.sync.dma_start(out=bias_rows[0:ROWS, :], in_=b_ih.rearrange("(a c) -> a c", a=ROWS))
        nc.sync.dma_start(out=bias_rows[ROWS : 2 * ROWS, :], in_=b_hh.rearrange("(a c) -> a c", a=ROWS))

        ident_bf = keep.tile([P, P], BF16)
        make_identity(nc, ident_bf[:])
        ident_f32 = keep.tile([P, P], F32)
        make_identity(nc, ident_f32[:])

        pick = keep.tile([P, 4, ROWS], BF16)
        nc.vector.tensor_add(out=pick[:, SUM, :], in0=ident_bf[:, 0:ROWS], in1=ident_bf[:, ROWS : 2 * ROWS])
        nc.vector.tensor_scalar_mul(out=pick[:, MINUS_SUM, :], in0=pick[:, SUM, :], scalar1=-1.0)
        nc.vector.tensor_copy(out=pick[:, B_IH : B_HH + 1, :], in_=ident_bf[:, 0 : 2 * ROWS].rearrange("p (k a) -> p k a", k=2))
        ones = keep.tile([P, P], BF16)
        nc.gpsimd.memset(ones[:], 1.0)
        bias_diag = keep.tile([P, PACK, P], BF16)
        for t in range(PACK):
            nc.vector.tensor_scalar_mul(out=bias_diag[:, t, :], in0=ident_bf[:], scalar1=b_emb_sb[:, t : t + 1])

        nc.scalar.activation(out=warm[:], in_=warm[:], func=ACT.Sigmoid)

        w_t_ps = psum.tile([P, PACK, P], BF16, tag="bank")
        for t in range(PACK):
            nc.tensor.transpose(w_t_ps[:, t, :], w_sb[:, t, :], ident_bf[:])
        w_t = keep.tile([P, PACK, P], BF16)
        nc.vector.tensor_copy(out=w_t[:], in_=w_t_ps[:])

        x_t = keep.tile([P, BATCH, PER_BATCH, P], BF16)

        def transpose_x(b, on_scalar):
            x_t_ps = psum.tile([P, PER_BATCH, P], BF16, tag="bank")
            for n in range(PER_BATCH):
                nc.tensor.transpose(x_t_ps[:, n, :], x_sb[:, b, n, :], ident_bf[:])
            if on_scalar:
                nc.scalar.copy(out=x_t[:, b], in_=x_t_ps[:])
            else:
                nc.vector.tensor_copy(out=x_t[:, b], in_=x_t_ps[:])

        grouped = keep.tile([P, GROUPS, P, PACK], BF16, align_bytes=64)
        emb_codes = keep.tile([P, GROUPS * P], U32, align_bytes=64)
        emb_plane = keep.tile([P, GROUPS * P], U8, align_bytes=64)

        def embed_group(g):
            emb_ps = psum.tile([P, PACK, P], F32, tag="bank")
            if g in SCALAR_EMBEDS:
                for t in range(PACK):
                    nc.tensor.matmul(emb_ps[:, t, :], lhsT=w_t[:, t, :], rhs=x_t[:, batch_of(g), n_of(g), :], start=True, stop=False)
                    nc.tensor.matmul(emb_ps[:, t, :], lhsT=bias_diag[:, t, :], rhs=ones[:], start=False, stop=True)
                nc.scalar.copy(out=grouped[:, g], in_=emb_ps[:].rearrange("p t s -> p s t"))
                return
            for t in range(PACK):
                nc.tensor.matmul(emb_ps[:, t, :], lhsT=w_t[:, t, :], rhs=x_t[:, batch_of(g), n_of(g), :], start=True, stop=True)
            nc.vector.tensor_tensor(
                out=grouped[:, g],
                in0=emb_ps[:].rearrange("p t s -> p s t"),
                in1=b_emb_sb[:].unsqueeze(1).to_broadcast([P, P, PACK]),
                op=ALU.add,
            )

        def quantise_groups(first, count):
            cols = slice(first * P, (first + count) * P)
            nc.vector.quantize_mx(
                out=emb_codes[:, cols].bitcast(FP8X4),
                scales=emb_plane[:, cols],
                in_=grouped[:, first : first + count].rearrange("p g s t -> p (g s t)"),
            )

        def quantise_chunk(c):
            first, count = CHUNK_FIRST[c], CHUNK_GROUPS[c]
            if c > 0:
                quantise_groups(first, count)
                return
            for g in range(first, first + count):
                quantise_groups(g, 1)

        def quantise_behind(g):
            for c in range(len(CHUNK_GROUPS)):
                if g == CHUNK_FIRST[c] + CHUNK_GROUPS[c] - 1:
                    quantise_chunk(c)

        def embed_and_quantise(g):
            embed_group(g)
            quantise_behind(g)

        bias_cols = keep.tile([P, PER_ROW, 4 * ROWS], F32)

        def gate_biases():
            bias_ps = psum.tile([P, PER_ROW, 4 * ROWS], F32, tag="bank")
            for k in range(PER_ROW):
                nc.tensor.matmul(
                    bias_ps[:, k, :], lhsT=bias_rows[:, k * P : (k + 1) * P], rhs=pick[:].rearrange("p k a -> p (k a)"), start=True, stop=True
                )
            nc.scalar.copy(out=bias_cols[:], in_=bias_ps[:])

        def bias_col(kind, gate, j):
            m = gate * TILES + j
            column = kind * ROWS + m // PER_ROW
            return bias_cols[:, m % PER_ROW, column : column + 1]

        transpose_x(0, on_scalar=True)
        transpose_x(1, on_scalar=False)
        transpose_x(2, on_scalar=True)
        for g in range(EMBEDS_AHEAD):
            if g == 3:
                gate_biases()
            embed_and_quantise(g)


        def columns_of(c):
            return slice(CHUNK_FIRST[c] * P, (CHUNK_FIRST[c] + CHUNK_GROUPS[c]) * P)

        def gate_pass(c, gate, j):
            m = gate * TILES + j
            gate_ps = psum.tile([P, CHUNK_GROUPS[c] * P], F32, tag="bank")
            nc.tensor.matmul_mx(
                out=gate_ps[:],
                lhsT=w_words[:, 2 * P * m : 2 * P * (m + 1)].bitcast(FP4X4),
                lhsT_scale=w_plane[:, P * m : P * (m + 1)],
                rhs=emb_codes[:, columns_of(c)].bitcast(FP8X4),
                rhs_scale=emb_plane[:, columns_of(c)],
                start=True,
                stop=True,
            )
            return gate_ps

        halves_of = {}
        h_t = keep.tile([P, TILES, GROUPS * P], F32)

        def gates(c, j):
            width = CHUNK_GROUPS[c] * P
            r_ps = gate_pass(c, R, j)
            z_ps = gate_pass(c, Z, j)
            n_ps = gate_pass(c, N, j)
            r_sb = work.tile([P, width], F32)
            nc.scalar.activation(out=r_sb[:], in_=r_ps[:], func=ACT.Sigmoid, bias=bias_col(SUM, R, j), scale=1.0)
            one_minus_z = work.tile([P, width], F32)
            nc.scalar.activation(
                out=one_minus_z[:], in_=z_ps[:], func=ACT.Sigmoid, bias=bias_col(MINUS_SUM, Z, j), scale=-1.0
            )
            pre_n = work.tile([P, width], F32)
            nc.vector.scalar_tensor_tensor(
                out=pre_n[:], in0=r_sb[:], scalar=bias_col(B_HH, N, j), in1=n_ps[:], op0=ALU.mult, op1=ALU.add
            )
            halves_of[(c, j)] = (one_minus_z, pre_n)

        n_of_step = {}

        def tanh(step):
            c, j = step // TILES, step % TILES
            n_sb = work.tile([P, CHUNK_GROUPS[c] * P], F32)
            nc.scalar.activation(
                out=n_sb[:], in_=halves_of[(c, j)][1][:], func=ACT.Tanh, bias=bias_col(B_IH, N, j), scale=1.0
            )
            n_of_step[step] = n_sb

        def product(step, engine):
            c, j = step // TILES, step % TILES
            engine.tensor_mul(out=h_t[:, j, columns_of(c)], in0=halves_of[(c, j)][0][:], in1=n_of_step[step][:])

        out_sb = keep.tile([P, GROUPS, HID], F32)
        out_rows = out_0.rearrange("b s h -> (b s) h")

        def store_rows(g, count, cols):
            b, n = batch_of(g), n_of(g)
            if n == PER_BATCH - 1:
                if b < BATCH - 1:
                    top = b * (STEPS - 1)
                    rows = out_rows[top : top + STEPS].rearrange("(p n) h -> p n h", n=PER_BATCH)
                    nc.sync.dma_start(out=rows[:, n, cols], in_=out_sb[:, g, cols])
                else:
                    for first, count_p in RAGGED_PIECES:
                        nc.sync.dma_start(
                            out=out_0[b, PER_BATCH * first + n : PER_BATCH * (first + count_p) : PER_BATCH, cols],
                            in_=out_sb[first : first + count_p, g, cols],
                        )
                nc.sync.dma_start(out=out_1[0, b : b + 1, cols], in_=out_sb[P - 1 : P, g, cols])
            elif count == 1:
                nc.sync.dma_start(out=out_0[b, n : STEPS - 1 : PER_BATCH, cols], in_=out_sb[:, g, cols])
            else:
                back = 1 if b == BATCH - 1 else 0
                top = b * (STEPS - 1) - back
                rows = out_rows[top : top + STEPS].rearrange("(p n) h -> p n h", n=PER_BATCH)
                nc.sync.dma_start(out=rows[:, n + back : n + back + count, cols], in_=out_sb[:, g : g + count, cols])

        def store_chunk(c, cols):
            g, end = CHUNK_FIRST[c], CHUNK_FIRST[c] + CHUNK_GROUPS[c]
            while g < end:
                count = 1
                while (
                    g + count < end
                    and batch_of(g) == batch_of(g + count)
                    and n_of(g) + count == n_of(g + count) < PER_BATCH - 1
                ):
                    count += 1
                store_rows(g, count, cols)
                g += count

        def way_out(step, on_scalar):
            c, j = step // TILES, step % TILES
            first, count = CHUNK_FIRST[c], CHUNK_GROUPS[c]
            h_ps = psum.tile([P, count, P], F32, tag="bank")
            for i in range(count):
                nc.tensor.transpose(h_ps[:, i, :], h_t[:, j, (first + i) * P : (first + i + 1) * P], ident_f32[:])
            if on_scalar:
                nc.scalar.copy(out=out_sb[:, first : first + count, j * P : (j + 1) * P], in_=h_ps[:])
            else:
                nc.vector.tensor_copy(out=out_sb[:, first : first + count, j * P : (j + 1) * P], in_=h_ps[:])
            if j == TILES // 2 - 1:
                store_chunk(c, slice(0, HID // 2))
            elif j >= TILES // 2 and c >= len(CHUNK_GROUPS) - 2:
                store_chunk(c, slice(j * P, (j + 1) * P))
            elif j == TILES - 1:
                store_chunk(c, slice(HID // 2, HID))

        n_steps = len(CHUNK_GROUPS) * TILES
        last = len(CHUNK_GROUPS) - 1
        for step in range(n_steps):
            embedded = embed_in_step(step)
            if embedded < GROUPS:
                embed_group(embedded)
            gates(step // TILES, step % TILES)
            if embedded < GROUPS:
                quantise_behind(embedded)
            if step >= 1:
                tanh(step - 1)
                if step < n_steps - 1:
                    product(step - 1, nc.gpsimd)
            if step >= 4 and (step - 4) % 2 == 1 and step < n_steps - 1:
                way_out(step - 4 - 1, on_scalar=False)
                way_out(step - 4, on_scalar=False)

        way_out(n_steps - 6, on_scalar=False)
        product(n_steps - 2, nc.vector)
        tanh(n_steps - 1)
        way_out(n_steps - 5, on_scalar=True)
        product(n_steps - 1, nc.vector)
        for step in range(n_steps - 4, n_steps):
            way_out(step, on_scalar=(step % 2 == 1))
